import numpy as np
import ml_dtypes


def mxq(x, axis, fmt="e4m3"):
    dtype, down = {"e4m3": (ml_dtypes.float8_e4m3fn, 7), "e5m2": (ml_dtypes.float8_e5m2, 14)}[fmt]
    v = np.moveaxis(np.asarray(x, np.float32).astype(ml_dtypes.bfloat16).astype(np.float64), axis, -1)
    blocks = v.reshape(v.shape[:-1] + (-1, 32))
    amax = np.abs(blocks).max(-1, keepdims=True)
    byte = np.maximum(np.where(amax > 0, np.frexp(amax)[1] - 1 + 127, 0) - down, 1)
    scale = np.exp2(byte - 127.0)
    codes = (blocks / scale).astype(np.float32).astype(dtype).astype(np.float64)
    return np.moveaxis((codes * scale).reshape(v.shape), -1, axis)


WIDE = False


def mx_kscale(k):
    if not WIDE:
        return np.ones(k)
    levels = np.array([20, -20, 10, -10, 0])
    a = np.random.permutation(np.resize(levels, k // 512 * 4)).reshape(k // 512, 4)
    idx = np.arange(k)
    return np.exp2(a[idx // 512, idx % 128 // 32])


BF16 = ml_dtypes.bfloat16


def bf(x):
    return np.asarray(x, np.float32).astype(BF16)


def f64(x):
    return np.asarray(x).astype(np.float64)


B, S, D_IN, D_OUT, GROUP_SIZE = 4, 1024, 1024, 512, 128
EPS = 1e-8


def ternary_quantize_groupwise(w, group_size=GROUP_SIZE, eps=EPS):
    orig_shape = w.shape
    last = orig_shape[-1]
    pad = (-last) % group_size
    if pad > 0:
        w = np.pad(w, [(0, 0)] * (w.ndim - 1) + [(0, pad)])
    num_groups = w.shape[-1] // group_size
    wg = w.reshape(-1, num_groups, group_size)
    scale = np.maximum(np.mean(np.abs(wg), axis=-1, keepdims=True), eps)
    wn = wg / scale
    q = np.where(wn > 0.5, 1.0, np.where(wn < -0.5, -1.0, 0.0))
    wq = (q * scale).reshape(w.shape)
    if pad > 0:
        wq = wq[..., :last]
    return wq.reshape(orig_shape)


def quantize_with_ste(w_real, group_size=GROUP_SIZE):
    w_q = ternary_quantize_groupwise(w_real, group_size=group_size)
    return w_real + (w_q - w_real)


def setup_inputs():
    u = mx_kscale(D_OUT)
    bound_w = 2.0 / np.sqrt(D_IN)
    x = np.random.standard_normal((B, S, D_IN))
    weight = np.random.uniform(-bound_w, bound_w, (D_OUT, D_IN)) / u[:, None]
    bias = np.random.uniform(-0.5, 0.5, D_OUT)
    g = np.random.standard_normal((B, S, D_OUT)) * np.exp2(np.random.randint(-12, 1, (B, S, 1))) * 16.0 * u
    return {"x": bf(x), "weight": bf(weight), "bias": bf(bias), "grad_out": bf(g)}


def reference(x, weight, bias, grad_out):
    w_q = quantize_with_ste(f64(weight), group_size=GROUP_SIZE)
    return mxq(f64(grad_out), 2, "e5m2") @ mxq(w_q, 0, "e4m3")

@@ -1,0 +1,255 @@
+from contextlib import ExitStack
+
+import concourse.mybir as mybir
+from concourse.masks import make_identity
+
+F32 = mybir.dt.float32
+BF16 = mybir.dt.bfloat16
+I32 = mybir.dt.int32
+U32 = mybir.dt.uint32
+U8 = mybir.dt.uint8
+E4 = mybir.dt.float8_e4m3fn_x4
+E5 = mybir.dt.float8_e5m2_x4
+ALU = mybir.AluOpType
+ACT = mybir.ActivationFunctionType
+AX = mybir.AxisListType
+
+P = 128
+TOK = 4096
+D_OUT = 512
+D_IN = 1024
+GROUP = 128
+NG = D_IN // GROUP
+EPS = 1e-8
+I_SG = 4
+N_SG = TOK // (P * I_SG)
+N_PAIR = TOK // (2 * P)
+HALF = 512
+SL = 16
+
+FLOPS = 2 * TOK * D_OUT * D_IN
+BYTES = 2 * D_OUT * D_IN + 2 * TOK * D_OUT + 4 * TOK * D_IN
+
+
+def tile_bitlinear_t_kernel(tc, x, weight, bias, grad_out, out):
+    nc = tc.nc
+    gv = grad_out.flatten_outer_dims().rearrange("(s p i) k -> s p (i k)", p=P, i=I_SG)
+    ov = out.flatten_outer_dims().rearrange("(s p i) c -> s p i c", p=P, i=I_SG)
+    wv = weight.rearrange("(u q e) c -> u q e c", u=2, e=2)
+
+    with ExitStack() as ctx:
+        ctx.enter_context(tc.manual_schedule())
+        keep = ctx.enter_context(tc.tile_pool(name="keep", bufs=1))
+        ggp = ctx.enter_context(tc.tile_pool(name="ggp", bufs=4))
+        osp = ctx.enter_context(tc.tile_pool(name="osp", bufs=8))
+        psum = ctx.enter_context(tc.psum_pool(name="psum", bufs=1))
+
+        def bank(b, shape):
+            return psum.tile(shape, F32, name="pb%d" % b, tag="b%d" % b)
+
+        w_sb = keep.tile([P, 4, D_IN], BF16, name="w_sb")
+        for h in range(2):
+            for u in range(2):
+                nc.sync.dma_start(
+                    out=w_sb[:, 2 * u : 2 * u + 2, h * HALF : (h + 1) * HALF],
+                    in_=wv[u][:, :, h * HALF : (h + 1) * HALF],
+                )
+        g_sb = []
+        for s in range(N_SG):
+            g_t = keep.tile([P, I_SG * D_OUT], BF16, name="g%d" % s)
+            nc.sync.dma_start(out=g_t[:], in_=gv[s])
+            g_sb.append(g_t)
+
+        ident_b = keep.tile([P, P], BF16, name="ident_b")
+        make_identity(nc, ident_b[:])
+        ident_f = keep.tile([P, P], F32, name="ident_f")
+        make_identity(nc, ident_f[:])
+        neg_b = keep.tile([P, P], BF16, name="neg_b")
+        nc.vector.tensor_scalar_mul(out=neg_b[:], in0=ident_b[:], scalar1=-1.0)
+
+        absw = keep.tile([P, 4, D_IN], BF16, name="absw")
+        sums = keep.tile([P, 2, 16], F32, name="sums")
+        scale = keep.tile([P, 2, 16], F32, name="scale")
+        thr = keep.tile([P, 2, 16], F32, name="thr")
+        nthr = keep.tile([P, 2, 16], F32, name="nthr")
+        a_sb = keep.tile([P, 4, D_IN], BF16, name="a_sb")
+        b_sb = keep.tile([P, 4, D_IN], BF16, name="b_sb")
+        wg = keep.tile([P, 4 * D_IN], BF16, name="wg", align_bytes=64)
+        w_codes = keep.tile([P, D_IN], U32, name="w_codes", align_bytes=64)
+        w_scales = keep.tile([P, D_IN], U8, name="w_scales", align_bytes=64)
+        g_codes = keep.tile([P, TOK], U32, name="g_codes", align_bytes=64)
+        g_scales = keep.tile([P, TOK], U8, name="g_scales", align_bytes=64)
+
+        w_int = w_sb[:].bitcast(I32)
+        absw_int = absw[:].bitcast(I32)
+        sum_banks = {}
+
+        def abs_vector(h, u):
+            nc.vector.tensor_single_scalar(
+                out=absw_int[:, 2 * u : 2 * u + 2, h * 256 : (h + 1) * 256],
+                in_=w_int[:, 2 * u : 2 * u + 2, h * 256 : (h + 1) * 256],
+                scalar=0x7FFF7FFF,
+                op=ALU.bitwise_and,
+            )
+
+        def abs_scalar(h, u):
+            nc.scalar.activation(
+                out=absw[:, 2 * u : 2 * u + 2, h * HALF : (h + 1) * HALF],
+                in_=w_sb[:, 2 * u : 2 * u + 2, h * HALF : (h + 1) * HALF],
+                func=ACT.Abs,
+            )
+
+        def fold(h, u):
+            if u == 0:
+                sum_banks[h] = bank(4 + h, [P, 4, 4, SL])
+            src = absw[:, 2 * u : 2 * u + 2, h * HALF : (h + 1) * HALF].rearrange(
+                "p t (g j i) -> p t g j i", g=4, i=SL
+            )
+            n_j = GROUP // SL
+            for j in range(n_j):
+                nc.tensor.matmul(
+                    out=sum_banks[h][:, 2 * u : 2 * u + 2, :, :],
+                    lhsT=ident_b[:],
+                    rhs=src[:, :, :, j, :],
+                    start=(j == 0),
+                    stop=(j == n_j - 1),
+                )
+
+        def thresholds(h):
+            nc.vector.tensor_reduce(
+                out=sums[:, h, :],
+                in_=sum_banks[h][:].rearrange("p t g i -> p (t g) i"),
+                axis=AX.X,
+                op=ALU.add,
+            )
+            nc.vector.tensor_scalar(
+                out=thr[:, h, :], in0=sums[:, h, :], scalar1=1.0 / 256, scalar2=EPS / 2,
+                op0=ALU.mult, op1=ALU.max,
+            )
+            nc.vector.tensor_scalar(
+                out=scale[:, h, :], in0=sums[:, h, :], scalar1=1.0 / 128, scalar2=EPS,
+                op0=ALU.mult, op1=ALU.max,
+            )
+            nc.vector.tensor_scalar(
+                out=nthr[:, h, :], in0=sums[:, h, :], scalar1=-1.0 / 256, scalar2=-EPS / 2,
+                op0=ALU.mult, op1=ALU.min,
+            )
+
+        def masks(g):
+            gs = slice(g * GROUP, (g + 1) * GROUP)
+            h = g // 4
+            for t in range(4):
+                c = t * 4 + g % 4
+                nc.vector.tensor_scalar(
+                    out=a_sb[:, t, gs], in0=w_sb[:, t, gs],
+                    scalar1=thr[:, h, c : c + 1], scalar2=scale[:, h, c : c + 1],
+                    op0=ALU.is_gt, op1=ALU.mult,
+                )
+                nc.vector.tensor_scalar(
+                    out=b_sb[:, t, gs], in0=w_sb[:, t, gs],
+                    scalar1=nthr[:, h, c : c + 1], scalar2=scale[:, h, c : c + 1],
+                    op0=ALU.is_lt, op1=ALU.mult,
+                )
+
+        WP_BANKS = (2, 3, 6, 7)
+
+        def join(g):
+            gs = slice(g * GROUP, (g + 1) * GROUP)
+            wp = bank(WP_BANKS[g % 4], [P, 4, GROUP])
+            nc.tensor.matmul(out=wp[:], lhsT=ident_b[:], rhs=a_sb[:, :, gs], start=True, stop=False)
+            nc.tensor.matmul(out=wp[:], lhsT=neg_b[:], rhs=b_sb[:, :, gs], start=False, stop=True)
+            nc.scalar.copy(
+                out=wg[:, g * 512 : (g + 1) * 512].rearrange("p (c t) -> p c t", t=4),
+                in_=wp[:].rearrange("p t c -> p c t"),
+            )
+
+        def quantise_w(h):
+            cols = slice(h * HALF, (h + 1) * HALF)
+            nc.vector.quantize_mx(
+                out=w_codes[:, cols].bitcast(E4),
+                scales=w_scales[:, cols],
+                in_=wg[:, h * 2048 : (h + 1) * 2048],
+            )
+
+        gg_tiles = {}
+
+        def transpose_pair(k):
+            gg = ggp.tile([P, 2 * D_OUT], BF16, name="gg", align_bytes=64)
+            gg_tiles[k] = gg
+            g_words = g_sb[k // 2][:].bitcast(F32)
+            gt = bank(k % 2, [P, 2, 2, P])
+            for j in range(2):
+                for u in range(2):
+                    c0 = ((k % 2) * 2 + j) * 256 + u * P
+                    nc.tensor.transpose(gt[:, j, u, :], g_words[:, c0 : c0 + P], ident_f[:])
+            nc.scalar.copy(
+                out=gg[:].bitcast(F32).rearrange("p (j r u) -> p j r u", j=2, u=2),
+                in_=gt[:].rearrange("p j u r -> p j r u"),
+            )
+
+        def quantise_pair(k):
+            cols = slice(k * 256, (k + 1) * 256)
+            nc.vector.quantize_mx(
+                out=g_codes[:, cols].bitcast(E5), scales=g_scales[:, cols], in_=gg_tiles[k][:]
+            )
+
+        PO_BANKS = (4, 5, 6, 7, 2, 3)
+
+        def multiply_pair(k, split_store):
+            ost = osp.tile([P, 2, D_IN], F32, name="ost")
+            s = k // 2
+            i0 = (k % 2) * 2
+            for j in range(2):
+                tcols = slice((2 * k + j) * P, (2 * k + j + 1) * P)
+                for h in range(2):
+                    hcols = slice(h * HALF, (h + 1) * HALF)
+                    po = bank(PO_BANKS[(4 * k + 2 * j + h) % 6], [P, HALF])
+                    nc.tensor.matmul_mx(
+                        out=po[:],
+                        lhsT=g_codes[:, tcols].bitcast(E5),
+                        lhsT_scale=g_scales[:, tcols],
+                        rhs=w_codes[:, hcols].bitcast(E4),
+                        rhs_scale=w_scales[:, hcols],
+                        start=True,
+                        stop=True,
+                    )
+                    if h == 0:
+                        nc.vector.tensor_copy(out=ost[:, j, hcols], in_=po[:])
+                    else:
+                        nc.scalar.copy(out=ost[:, j, hcols], in_=po[:])
+                if split_store:
+                    nc.sync.dma_start(out=ov[s][:, i0 + j : i0 + j + 1, :], in_=ost[:, j : j + 1, :])
+            if not split_store:
+                nc.sync.dma_start(out=ov[s][:, i0 : i0 + 2, :], in_=ost[:])
+
+        abs_vector(0, 0)
+        fold(0, 0)
+        abs_vector(0, 1)
+        fold(0, 1)
+        abs_vector(1, 0)
+        abs_scalar(1, 1)
+        fold(1, 0)
+        thresholds(0)
+        transpose_pair(0)
+        masks(0)
+        join(0)
+        fold(1, 1)
+        for g in range(1, 4):
+            masks(g)
+            join(g)
+        thresholds(1)
+        for g in range(4, NG):
+            masks(g)
+            join(g)
+        quantise_pair(0)
+        quantise_w(0)
+        transpose_pair(1)
+        quantise_w(1)
+        transpose_pair(2)
+        quantise_pair(1)
+        for k in range(N_PAIR):
+            if k + 3 < N_PAIR:
+                transpose_pair(k + 3)
+            multiply_pair(k, k == 0)
+            if k + 2 < N_PAIR:
+                quantise_pair(k + 2)

@@ -19,11 +19,9 @@ TOK = 4096
 D_OUT = 512
 D_IN = 1024
 GROUP = 128
-NG = D_IN // GROUP
 EPS = 1e-8
 I_SG = 4
 N_SG = TOK // (P * I_SG)
-N_PAIR = TOK // (2 * P)
 HALF = 512
 SL = 16
 
@@ -47,18 +45,31 @@ def tile_bitlinear_t_kernel(tc, x, weight, bias, grad_out, out):
         def bank(b, shape):
             return psum.tile(shape, F32, name="pb%d" % b, tag="b%d" % b)
 
-        w_sb = keep.tile([P, 4, D_IN], BF16, name="w_sb")
-        for h in range(2):
-            for u in range(2):
-                nc.sync.dma_start(
-                    out=w_sb[:, 2 * u : 2 * u + 2, h * HALF : (h + 1) * HALF],
-                    in_=wv[u][:, :, h * HALF : (h + 1) * HALF],
-                )
-        g_sb = []
-        for s in range(N_SG):
-            g_t = keep.tile([P, I_SG * D_OUT], BF16, name="g%d" % s)
-            nc.sync.dma_start(out=g_t[:], in_=gv[s])
-            g_sb.append(g_t)
+        w2 = [keep.tile([P, 2, 4, HALF], BF16, name="w2_%d" % h) for h in range(2)]
+        absw = [keep.tile([P, 4, HALF], BF16, name="absw%d" % h) for h in range(2)]
+        g_sb = [keep.tile([P, I_SG * D_OUT], BF16, name="g%d" % s) for s in range(N_SG)]
+
+        def load_w(h, u):
+            nc.sync.dma_start(
+                out=w2[h][:, 0, 2 * u : 2 * u + 2, :], in_=wv[u][:, :, h * HALF : (h + 1) * HALF]
+            )
+
+        def load_g(s, c0, c1):
+            nc.sync.dma_start(out=g_sb[s][:, c0:c1], in_=gv[s][:, c0:c1])
+
+        load_w(0, 0)
+        load_w(0, 1)
+        load_w(1, 0)
+        load_w(1, 1)
+        load_g(0, 0, 1024)
+        load_g(0, 1024, 2048)
+        load_g(1, 0, 2048)
+        load_g(2, 0, 2048)
+        load_g(3, 0, 2048)
+        load_g(4, 0, 2048)
+        load_g(5, 0, 2048)
+        load_g(6, 0, 2048)
+        load_g(7, 0, 2048)
 
         ident_b = keep.tile([P, P], BF16, name="ident_b")
         make_identity(nc, ident_b[:])
@@ -67,48 +78,57 @@ def tile_bitlinear_t_kernel(tc, x, weight, bias, grad_out, out):
         neg_b = keep.tile([P, P], BF16, name="neg_b")
         nc.vector.tensor_scalar_mul(out=neg_b[:], in0=ident_b[:], scalar1=-1.0)
 
-        absw = keep.tile([P, 4, D_IN], BF16, name="absw")
         sums = keep.tile([P, 2, 16], F32, name="sums")
         scale = keep.tile([P, 2, 16], F32, name="scale")
         thr = keep.tile([P, 2, 16], F32, name="thr")
-        nthr = keep.tile([P, 2, 16], F32, name="nthr")
-        a_sb = keep.tile([P, 4, D_IN], BF16, name="a_sb")
-        b_sb = keep.tile([P, 4, D_IN], BF16, name="b_sb")
+        ab = keep.tile([P, 8, 2, 4, GROUP], BF16, name="ab")
         wg = keep.tile([P, 4 * D_IN], BF16, name="wg", align_bytes=64)
         w_codes = keep.tile([P, D_IN], U32, name="w_codes", align_bytes=64)
         w_scales = keep.tile([P, D_IN], U8, name="w_scales", align_bytes=64)
         g_codes = keep.tile([P, TOK], U32, name="g_codes", align_bytes=64)
         g_scales = keep.tile([P, TOK], U8, name="g_scales", align_bytes=64)
 
-        w_int = w_sb[:].bitcast(I32)
-        absw_int = absw[:].bitcast(I32)
-        sum_banks = {}
+        banks = {}
+        gg_tiles = {}
+        ost_tiles = {}
 
-        def abs_vector(h, u):
+        def copy_on(eng, dst, src):
+            if eng == "V":
+                nc.vector.tensor_copy(out=dst, in_=src)
+            else:
+                nc.scalar.copy(out=dst, in_=src)
+
+        def absv(h, u):
             nc.vector.tensor_single_scalar(
-                out=absw_int[:, 2 * u : 2 * u + 2, h * 256 : (h + 1) * 256],
-                in_=w_int[:, 2 * u : 2 * u + 2, h * 256 : (h + 1) * 256],
+                out=absw[h][:].bitcast(I32)[:, 2 * u : 2 * u + 2, :],
+                in_=w2[h][:].bitcast(I32)[:, 0, 2 * u : 2 * u + 2, :],
                 scalar=0x7FFF7FFF,
                 op=ALU.bitwise_and,
             )
 
-        def abs_scalar(h, u):
+        def abss(h, u):
             nc.scalar.activation(
-                out=absw[:, 2 * u : 2 * u + 2, h * HALF : (h + 1) * HALF],
-                in_=w_sb[:, 2 * u : 2 * u + 2, h * HALF : (h + 1) * HALF],
-                func=ACT.Abs,
+                out=absw[h][:, 2 * u : 2 * u + 2, :], in_=w2[h][:, 0, 2 * u : 2 * u + 2, :], func=ACT.Abs
             )
 
-        def fold(h, u):
-            if u == 0:
-                sum_banks[h] = bank(4 + h, [P, 4, 4, SL])
-            src = absw[:, 2 * u : 2 * u + 2, h * HALF : (h + 1) * HALF].rearrange(
-                "p t (g j i) -> p t g j i", g=4, i=SL
+        def negv(h, u):
+            nc.vector.tensor_scalar_mul(
+                out=w2[h][:, 1, 2 * u : 2 * u + 2, :], in0=w2[h][:, 0, 2 * u : 2 * u + 2, :], scalar1=-1.0
             )
+
+        def negs(h, u):
+            nc.scalar.mul(
+                out=w2[h][:, 1, 2 * u : 2 * u + 2, :], in_=w2[h][:, 0, 2 * u : 2 * u + 2, :], mul=-1.0
+            )
+
+        def fold(h, u, b):
+            if u == 0:
+                banks["F%d" % h] = bank(b, [P, 4, 4, SL])
+            src = absw[h][:, 2 * u : 2 * u + 2, :].rearrange("p t (g j i) -> p t g j i", g=4, i=SL)
             n_j = GROUP // SL
             for j in range(n_j):
                 nc.tensor.matmul(
-                    out=sum_banks[h][:, 2 * u : 2 * u + 2, :, :],
+                    out=banks["F%d" % h][:, 2 * u : 2 * u + 2, :, :],
                     lhsT=ident_b[:],
                     rhs=src[:, :, :, j, :],
                     start=(j == 0),
@@ -118,7 +138,7 @@ def tile_bitlinear_t_kernel(tc, x, weight, bias, grad_out, out):
         def thresholds(h):
             nc.vector.tensor_reduce(
                 out=sums[:, h, :],
-                in_=sum_banks[h][:].rearrange("p t g i -> p (t g) i"),
+                in_=banks["F%d" % h][:].rearrange("p t g i -> p (t g) i"),
                 axis=AX.X,
                 op=ALU.add,
             )
@@ -130,40 +150,32 @@ def tile_bitlinear_t_kernel(tc, x, weight, bias, grad_out, out):
                 out=scale[:, h, :], in0=sums[:, h, :], scalar1=1.0 / 128, scalar2=EPS,
                 op0=ALU.mult, op1=ALU.max,
             )
-            nc.vector.tensor_scalar(
-                out=nthr[:, h, :], in0=sums[:, h, :], scalar1=-1.0 / 256, scalar2=-EPS / 2,
-                op0=ALU.mult, op1=ALU.min,
-            )
 
         def masks(g):
-            gs = slice(g * GROUP, (g + 1) * GROUP)
             h = g // 4
+            gs = slice((g % 4) * GROUP, (g % 4 + 1) * GROUP)
             for t in range(4):
                 c = t * 4 + g % 4
                 nc.vector.tensor_scalar(
-                    out=a_sb[:, t, gs], in0=w_sb[:, t, gs],
+                    out=ab[:, g, :, t, :], in0=w2[h][:, :, t, gs],
                     scalar1=thr[:, h, c : c + 1], scalar2=scale[:, h, c : c + 1],
                     op0=ALU.is_gt, op1=ALU.mult,
                 )
-                nc.vector.tensor_scalar(
-                    out=b_sb[:, t, gs], in0=w_sb[:, t, gs],
-                    scalar1=nthr[:, h, c : c + 1], scalar2=scale[:, h, c : c + 1],
-                    op0=ALU.is_lt, op1=ALU.mult,
-                )
 
-        WP_BANKS = (2, 3, 6, 7)
+        def joinpe(g, b):
+            wp = bank(b, [P, 4, GROUP])
+            banks["W%d" % g] = wp
+            nc.tensor.matmul(out=wp[:], lhsT=ident_b[:], rhs=ab[:, g, 0, :, :], start=True, stop=False)
+            nc.tensor.matmul(out=wp[:], lhsT=neg_b[:], rhs=ab[:, g, 1, :, :], start=False, stop=True)
 
-        def join(g):
-            gs = slice(g * GROUP, (g + 1) * GROUP)
-            wp = bank(WP_BANKS[g % 4], [P, 4, GROUP])
-            nc.tensor.matmul(out=wp[:], lhsT=ident_b[:], rhs=a_sb[:, :, gs], start=True, stop=False)
-            nc.tensor.matmul(out=wp[:], lhsT=neg_b[:], rhs=b_sb[:, :, gs], start=False, stop=True)
-            nc.scalar.copy(
-                out=wg[:, g * 512 : (g + 1) * 512].rearrange("p (c t) -> p c t", t=4),
-                in_=wp[:].rearrange("p t c -> p c t"),
+        def joinev(g, eng):
+            copy_on(
+                eng,
+                wg[:, g * 512 : (g + 1) * 512].rearrange("p (c t) -> p c t", t=4),
+                banks["W%d" % g][:].rearrange("p t c -> p c t"),
             )
 
-        def quantise_w(h):
+        def qw(h):
             cols = slice(h * HALF, (h + 1) * HALF)
             nc.vector.quantize_mx(
                 out=w_codes[:, cols].bitcast(E4),
@@ -171,85 +183,298 @@ def tile_bitlinear_t_kernel(tc, x, weight, bias, grad_out, out):
                 in_=wg[:, h * 2048 : (h + 1) * 2048],
             )
 
-        gg_tiles = {}
+        def qwq(i):
+            cols = slice(i * 256, (i + 1) * 256)
+            nc.vector.quantize_mx(
+                out=w_codes[:, cols].bitcast(E4),
+                scales=w_scales[:, cols],
+                in_=wg[:, i * 1024 : (i + 1) * 1024],
+            )
 
-        def transpose_pair(k):
-            gg = ggp.tile([P, 2 * D_OUT], BF16, name="gg", align_bytes=64)
-            gg_tiles[k] = gg
+        def tpe(k, b):
             g_words = g_sb[k // 2][:].bitcast(F32)
-            gt = bank(k % 2, [P, 2, 2, P])
+            gt = bank(b, [P, 2, 2, P])
+            banks["T%d" % k] = gt
             for j in range(2):
                 for u in range(2):
                     c0 = ((k % 2) * 2 + j) * 256 + u * P
                     nc.tensor.transpose(gt[:, j, u, :], g_words[:, c0 : c0 + P], ident_f[:])
-            nc.scalar.copy(
-                out=gg[:].bitcast(F32).rearrange("p (j r u) -> p j r u", j=2, u=2),
-                in_=gt[:].rearrange("p j u r -> p j r u"),
+
+        def tev(k, eng):
+            gg = ggp.tile([P, 2 * D_OUT], BF16, name="gg", align_bytes=64)
+            gg_tiles[k] = gg
+            copy_on(
+                eng,
+                gg[:].bitcast(F32).rearrange("p (j r u) -> p j r u", j=2, u=2),
+                banks["T%d" % k][:].rearrange("p j u r -> p j r u"),
             )
 
-        def quantise_pair(k):
+        def qg(k):
             cols = slice(k * 256, (k + 1) * 256)
             nc.vector.quantize_mx(
                 out=g_codes[:, cols].bitcast(E5), scales=g_scales[:, cols], in_=gg_tiles[k][:]
             )
 
-        PO_BANKS = (4, 5, 6, 7, 2, 3)
+        def mx(t, h, b):
+            tcols = slice(t * P, (t + 1) * P)
+            hcols = slice(h * HALF, (h + 1) * HALF)
+            po = bank(b, [P, HALF])
+            banks["O%d_%d" % (t, h)] = po
+            nc.tensor.matmul_mx(
+                out=po[:],
+                lhsT=g_codes[:, tcols].bitcast(E5),
+                lhsT_scale=g_scales[:, tcols],
+                rhs=w_codes[:, hcols].bitcast(E4),
+                rhs_scale=w_scales[:, hcols],
+                start=True,
+                stop=True,
+            )
 
-        def multiply_pair(k, split_store):
-            ost = osp.tile([P, 2, D_IN], F32, name="ost")
-            s = k // 2
-            i0 = (k % 2) * 2
-            for j in range(2):
-                tcols = slice((2 * k + j) * P, (2 * k + j + 1) * P)
-                for h in range(2):
-                    hcols = slice(h * HALF, (h + 1) * HALF)
-                    po = bank(PO_BANKS[(4 * k + 2 * j + h) % 6], [P, HALF])
-                    nc.tensor.matmul_mx(
-                        out=po[:],
-                        lhsT=g_codes[:, tcols].bitcast(E5),
-                        lhsT_scale=g_scales[:, tcols],
-                        rhs=w_codes[:, hcols].bitcast(E4),
-                        rhs_scale=w_scales[:, hcols],
-                        start=True,
-                        stop=True,
-                    )
-                    if h == 0:
-                        nc.vector.tensor_copy(out=ost[:, j, hcols], in_=po[:])
-                    else:
-                        nc.scalar.copy(out=ost[:, j, hcols], in_=po[:])
-                if split_store:
-                    nc.sync.dma_start(out=ov[s][:, i0 + j : i0 + j + 1, :], in_=ost[:, j : j + 1, :])
-            if not split_store:
-                nc.sync.dma_start(out=ov[s][:, i0 : i0 + 2, :], in_=ost[:])
+        def eo(t, h, eng):
+            grp = t // 2
+            if grp not in ost_tiles:
+                ost_tiles[grp] = osp.tile([P, 2, D_IN], F32, name="ost")
+            copy_on(eng, ost_tiles[grp][:, t % 2, h * HALF : (h + 1) * HALF], banks["O%d_%d" % (t, h)][:])
 
-        abs_vector(0, 0)
-        fold(0, 0)
-        abs_vector(0, 1)
-        fold(0, 1)
-        abs_vector(1, 0)
-        abs_scalar(1, 1)
-        fold(1, 0)
+        def store(t0, n, c0, c1):
+            grp = t0 // 2
+            nc.sync.dma_start(
+                out=ov[t0 // I_SG][:, t0 % I_SG : t0 % I_SG + n, c0:c1],
+                in_=ost_tiles[grp][:, t0 % 2 : t0 % 2 + n, c0:c1],
+            )
+
+        negs(0, 0)
+        absv(0, 0)
+        fold(0, 0, 4)
+        absv(0, 1)
+        fold(0, 1, 4)
+        negs(0, 1)
+        absv(1, 0)
+        fold(1, 0, 5)
+        absv(1, 1)
+        fold(1, 1, 5)
         thresholds(0)
-        transpose_pair(0)
+        negs(1, 0)
+        tpe(0, 0)
         masks(0)
-        join(0)
-        fold(1, 1)
-        for g in range(1, 4):
-            masks(g)
-            join(g)
+        joinpe(0, 2)
+        masks(1)
+        joinpe(1, 3)
+        negv(1, 1)
+        masks(2)
+        joinev(0, "S")
+        joinpe(2, 6)
         thresholds(1)
-        for g in range(4, NG):
-            masks(g)
-            join(g)
-        quantise_pair(0)
-        quantise_w(0)
-        transpose_pair(1)
-        quantise_w(1)
-        transpose_pair(2)
-        quantise_pair(1)
-        for k in range(N_PAIR):
-            if k + 3 < N_PAIR:
-                transpose_pair(k + 3)
-            multiply_pair(k, k == 0)
-            if k + 2 < N_PAIR:
-                quantise_pair(k + 2)
+        masks(3)
+        joinev(1, "S")
+        joinpe(3, 7)
+        masks(4)
+        joinev(2, "S")
+        joinpe(4, 2)
+        masks(5)
+        joinev(3, "S")
+        joinpe(5, 3)
+        masks(6)
+        joinpe(6, 6)
+        masks(7)
+        joinev(4, "S")
+        joinpe(7, 7)
+        tev(0, "V")
+        qwq(0)
+        joinev(5, "S")
+        qg(0)
+        qwq(1)
+        joinev(6, "S")
+        tpe(1, 1)
+        qwq(2)
+        joinev(7, "S")
+        mx(0, 0, 4)
+        mx(1, 0, 5)
+        tpe(2, 0)
+        qwq(3)
+        tev(1, "S")
+        eo(0, 0, "V")
+        eo(1, 0, "S")
+        qg(1)
+        mx(0, 1, 2)
+        mx(1, 1, 3)
+        eo(0, 1, "V")
+        store(0, 1, 0, D_IN)
+        eo(1, 1, "S")
+        store(1, 1, 0, D_IN)
+        mx(2, 0, 6)
+        mx(2, 1, 7)
+        mx(3, 0, 4)
+        mx(3, 1, 5)
+        tpe(3, 1)
+        eo(2, 0, "V")
+        eo(2, 1, "S")
+        tev(2, "S")
+        eo(3, 0, "V")
+        qg(2)
+        eo(3, 1, "S")
+        store(2, 2, 0, D_IN)
+        tev(3, "S")
+        qg(3)
+        tpe(4, 0)
+        tev(4, "S")
+        mx(4, 0, 2)
+        eo(4, 0, "V")
+        mx(4, 1, 3)
+        eo(4, 1, "S")
+        mx(5, 0, 6)
+        eo(5, 0, "V")
+        mx(5, 1, 7)
+        eo(5, 1, "S")
+        store(4, 2, 0, D_IN)
+        qg(4)
+        tpe(5, 1)
+        tev(5, "S")
+        mx(6, 0, 4)
+        eo(6, 0, "V")
+        mx(6, 1, 5)
+        eo(6, 1, "S")
+        mx(7, 0, 2)
+        eo(7, 0, "V")
+        mx(7, 1, 3)
+        eo(7, 1, "S")
+        store(6, 2, 0, D_IN)
+        qg(5)
+        tpe(6, 0)
+        tev(6, "S")
+        mx(8, 0, 6)
+        eo(8, 0, "V")
+        mx(8, 1, 7)
+        eo(8, 1, "S")
+        mx(9, 0, 4)
+        eo(9, 0, "V")
+        mx(9, 1, 5)
+        eo(9, 1, "S")
+        store(8, 2, 0, D_IN)
+        qg(6)
+        tpe(7, 1)
+        tev(7, "S")
+        mx(10, 0, 2)
+        eo(10, 0, "V")
+        mx(10, 1, 3)
+        eo(10, 1, "S")
+        mx(11, 0, 6)
+        eo(11, 0, "V")
+        mx(11, 1, 7)
+        eo(11, 1, "S")
+        store(10, 2, 0, D_IN)
+        qg(7)
+        tpe(8, 0)
+        tev(8, "S")
+        mx(12, 0, 4)
+        eo(12, 0, "V")
+        mx(12, 1, 5)
+        eo(12, 1, "S")
+        mx(13, 0, 2)
+        eo(13, 0, "V")
+        mx(13, 1, 3)
+        eo(13, 1, "S")
+        store(12, 2, 0, D_IN)
+        qg(8)
+        tpe(9, 1)
+        tev(9, "S")
+        mx(14, 0, 6)
+        eo(14, 0, "V")
+        mx(14, 1, 7)
+        eo(14, 1, "S")
+        mx(15, 0, 4)
+        eo(15, 0, "V")
+        mx(15, 1, 5)
+        eo(15, 1, "S")
+        store(14, 2, 0, D_IN)
+        qg(9)
+        tpe(10, 0)
+        tev(10, "S")
+        mx(16, 0, 2)
+        eo(16, 0, "V")
+        mx(16, 1, 3)
+        eo(16, 1, "S")
+        mx(17, 0, 6)
+        eo(17, 0, "V")
+        mx(17, 1, 7)
+        eo(17, 1, "S")
+        store(16, 2, 0, D_IN)
+        qg(10)
+        tpe(11, 1)
+        tev(11, "S")
+        mx(18, 0, 4)
+        eo(18, 0, "V")
+        mx(18, 1, 5)
+        eo(18, 1, "S")
+        mx(19, 0, 2)
+        eo(19, 0, "V")
+        mx(19, 1, 3)
+        eo(19, 1, "S")
+        store(18, 2, 0, D_IN)
+        qg(11)
+        tpe(12, 0)
+        tev(12, "S")
+        mx(20, 0, 6)
+        eo(20, 0, "V")
+        mx(20, 1, 7)
+        eo(20, 1, "S")
+        mx(21, 0, 4)
+        eo(21, 0, "V")
+        mx(21, 1, 5)
+        eo(21, 1, "S")
+        store(20, 2, 0, D_IN)
+        qg(12)
+        tpe(13, 1)
+        tev(13, "S")
+        mx(22, 0, 2)
+        eo(22, 0, "V")
+        mx(22, 1, 3)
+        eo(22, 1, "S")
+        mx(23, 0, 6)
+        eo(23, 0, "V")
+        mx(23, 1, 7)
+        eo(23, 1, "S")
+        store(22, 2, 0, D_IN)
+        qg(13)
+        tpe(14, 0)
+        tev(14, "S")
+        mx(24, 0, 4)
+        eo(24, 0, "V")
+        mx(24, 1, 5)
+        eo(24, 1, "S")
+        mx(25, 0, 2)
+        eo(25, 0, "V")
+        mx(25, 1, 3)
+        eo(25, 1, "S")
+        store(24, 2, 0, D_IN)
+        qg(14)
+        tpe(15, 1)
+        tev(15, "S")
+        mx(26, 0, 6)
+        eo(26, 0, "V")
+        mx(26, 1, 7)
+        eo(26, 1, "S")
+        mx(27, 0, 4)
+        eo(27, 0, "V")
+        mx(27, 1, 5)
+        eo(27, 1, "S")
+        store(26, 2, 0, D_IN)
+        qg(15)
+        mx(28, 0, 2)
+        eo(28, 0, "V")
+        mx(28, 1, 3)
+        eo(28, 1, "S")
+        mx(29, 0, 6)
+        eo(29, 0, "V")
+        mx(29, 1, 7)
+        eo(29, 1, "S")
+        store(28, 2, 0, D_IN)
+        mx(30, 0, 4)
+        eo(30, 0, "V")
+        mx(30, 1, 5)
+        eo(30, 1, "S")
+        mx(31, 0, 2)
+        eo(31, 0, "V")
+        mx(31, 1, 3)
+        eo(31, 1, "S")
+        store(30, 2, 0, D_IN)

@@ -46,7 +46,6 @@ def tile_bitlinear_t_kernel(tc, x, weight, bias, grad_out, out):
             return psum.tile(shape, F32, name="pb%d" % b, tag="b%d" % b)
 
         w2 = [keep.tile([P, 2, 4, HALF], BF16, name="w2_%d" % h) for h in range(2)]
-        absw = [keep.tile([P, 4, HALF], BF16, name="absw%d" % h) for h in range(2)]
         g_sb = [keep.tile([P, I_SG * D_OUT], BF16, name="g%d" % s) for s in range(N_SG)]
 
         def load_w(h, u):
@@ -75,6 +74,8 @@ def tile_bitlinear_t_kernel(tc, x, weight, bias, grad_out, out):
         make_identity(nc, ident_b[:])
         ident_f = keep.tile([P, P], F32, name="ident_f")
         make_identity(nc, ident_f[:])
+        two_b = keep.tile([P, P], BF16, name="two_b")
+        nc.vector.tensor_scalar_mul(out=two_b[:], in0=ident_b[:], scalar1=2.0)
         neg_b = keep.tile([P, P], BF16, name="neg_b")
         nc.vector.tensor_scalar_mul(out=neg_b[:], in0=ident_b[:], scalar1=-1.0)
 
@@ -100,7 +101,7 @@ def tile_bitlinear_t_kernel(tc, x, weight, bias, grad_out, out):
 
         def absv(h, u):
             nc.vector.tensor_single_scalar(
-                out=absw[h][:].bitcast(I32)[:, 2 * u : 2 * u + 2, :],
+                out=w2[h][:].bitcast(I32)[:, 1, 2 * u : 2 * u + 2, :],
                 in_=w2[h][:].bitcast(I32)[:, 0, 2 * u : 2 * u + 2, :],
                 scalar=0x7FFF7FFF,
                 op=ALU.bitwise_and,
@@ -108,23 +109,13 @@ def tile_bitlinear_t_kernel(tc, x, weight, bias, grad_out, out):
 
         def abss(h, u):
             nc.scalar.activation(
-                out=absw[h][:, 2 * u : 2 * u + 2, :], in_=w2[h][:, 0, 2 * u : 2 * u + 2, :], func=ACT.Abs
-            )
-
-        def negv(h, u):
-            nc.vector.tensor_scalar_mul(
-                out=w2[h][:, 1, 2 * u : 2 * u + 2, :], in0=w2[h][:, 0, 2 * u : 2 * u + 2, :], scalar1=-1.0
-            )
-
-        def negs(h, u):
-            nc.scalar.mul(
-                out=w2[h][:, 1, 2 * u : 2 * u + 2, :], in_=w2[h][:, 0, 2 * u : 2 * u + 2, :], mul=-1.0
+                out=w2[h][:, 1, 2 * u : 2 * u + 2, :], in_=w2[h][:, 0, 2 * u : 2 * u + 2, :], func=ACT.Abs
             )
 
         def fold(h, u, b):
             if u == 0:
                 banks["F%d" % h] = bank(b, [P, 4, 4, SL])
-            src = absw[h][:, 2 * u : 2 * u + 2, :].rearrange("p t (g j i) -> p t g j i", g=4, i=SL)
+            src = w2[h][:, 1, 2 * u : 2 * u + 2, :].rearrange("p t (g j i) -> p t g j i", g=4, i=SL)
             n_j = GROUP // SL
             for j in range(n_j):
                 nc.tensor.matmul(
@@ -165,7 +156,7 @@ def tile_bitlinear_t_kernel(tc, x, weight, bias, grad_out, out):
         def joinpe(g, b):
             wp = bank(b, [P, 4, GROUP])
             banks["W%d" % g] = wp
-            nc.tensor.matmul(out=wp[:], lhsT=ident_b[:], rhs=ab[:, g, 0, :, :], start=True, stop=False)
+            nc.tensor.matmul(out=wp[:], lhsT=two_b[:], rhs=ab[:, g, 0, :, :], start=True, stop=False)
             nc.tensor.matmul(out=wp[:], lhsT=neg_b[:], rhs=ab[:, g, 1, :, :], start=False, stop=True)
 
         def joinev(g, eng):
@@ -243,237 +234,233 @@ def tile_bitlinear_t_kernel(tc, x, weight, bias, grad_out, out):
                 in_=ost_tiles[grp][:, t0 % 2 : t0 % 2 + n, c0:c1],
             )
 
-        negs(0, 0)
         absv(0, 0)
-        fold(0, 0, 4)
+        fold(0, 0, 0)
         absv(0, 1)
-        fold(0, 1, 4)
-        negs(0, 1)
+        fold(0, 1, 0)
         absv(1, 0)
-        fold(1, 0, 5)
-        absv(1, 1)
-        fold(1, 1, 5)
+        fold(1, 0, 1)
+        abss(1, 1)
         thresholds(0)
-        negs(1, 0)
-        tpe(0, 0)
+        tpe(0, 2)
         masks(0)
-        joinpe(0, 2)
+        joinpe(0, 3)
+        tev(0, "S")
         masks(1)
-        joinpe(1, 3)
-        negv(1, 1)
-        masks(2)
+        fold(1, 1, 1)
+        joinpe(1, 4)
         joinev(0, "S")
-        joinpe(2, 6)
-        thresholds(1)
-        masks(3)
+        masks(2)
+        joinpe(2, 5)
         joinev(1, "S")
-        joinpe(3, 7)
-        masks(4)
+        masks(3)
+        joinpe(3, 6)
         joinev(2, "S")
-        joinpe(4, 2)
-        masks(5)
+        thresholds(1)
+        masks(4)
+        joinpe(4, 7)
         joinev(3, "S")
-        joinpe(5, 3)
-        masks(6)
-        joinpe(6, 6)
-        masks(7)
+        masks(5)
+        joinpe(5, 0)
         joinev(4, "S")
-        joinpe(7, 7)
-        tev(0, "V")
-        qwq(0)
+        masks(6)
+        joinpe(6, 2)
         joinev(5, "S")
+        masks(7)
+        joinpe(7, 3)
+        joinev(7, "S")
+        qwq(0)
+        tpe(1, 4)
+        tev(1, "S")
+        tpe(2, 5)
         qg(0)
         qwq(1)
-        joinev(6, "S")
-        tpe(1, 1)
+        mx(0, 0, 1)
+        joinev(6, "V")
         qwq(2)
-        joinev(7, "S")
-        mx(0, 0, 4)
-        mx(1, 0, 5)
-        tpe(2, 0)
         qwq(3)
-        tev(1, "S")
-        eo(0, 0, "V")
-        eo(1, 0, "S")
+        mx(0, 1, 6)
+        mx(1, 0, 7)
+        eo(0, 0, "S")
         qg(1)
-        mx(0, 1, 2)
-        mx(1, 1, 3)
         eo(0, 1, "V")
+        mx(1, 1, 0)
+        eo(1, 0, "S")
         store(0, 1, 0, D_IN)
+        mx(2, 0, 3)
+        tev(2, "V")
+        mx(2, 1, 4)
         eo(1, 1, "S")
         store(1, 1, 0, D_IN)
-        mx(2, 0, 6)
-        mx(2, 1, 7)
-        mx(3, 0, 4)
-        mx(3, 1, 5)
-        tpe(3, 1)
+        mx(3, 0, 2)
         eo(2, 0, "V")
-        eo(2, 1, "S")
-        tev(2, "S")
-        eo(3, 0, "V")
         qg(2)
+        mx(3, 1, 1)
+        eo(2, 1, "S")
+        eo(3, 0, "V")
         eo(3, 1, "S")
         store(2, 2, 0, D_IN)
-        tev(3, "S")
+        tpe(3, 6)
+        tev(3, "V")
         qg(3)
-        tpe(4, 0)
+        tpe(4, 7)
         tev(4, "S")
-        mx(4, 0, 2)
+        mx(4, 0, 5)
         eo(4, 0, "V")
-        mx(4, 1, 3)
+        mx(4, 1, 0)
         eo(4, 1, "S")
-        mx(5, 0, 6)
+        mx(5, 0, 3)
         eo(5, 0, "V")
-        mx(5, 1, 7)
+        mx(5, 1, 4)
         eo(5, 1, "S")
         store(4, 2, 0, D_IN)
         qg(4)
-        tpe(5, 1)
+        tpe(5, 2)
         tev(5, "S")
-        mx(6, 0, 4)
+        mx(6, 0, 1)
         eo(6, 0, "V")
-        mx(6, 1, 5)
+        mx(6, 1, 6)
         eo(6, 1, "S")
-        mx(7, 0, 2)
+        mx(7, 0, 7)
         eo(7, 0, "V")
-        mx(7, 1, 3)
+        mx(7, 1, 5)
         eo(7, 1, "S")
         store(6, 2, 0, D_IN)
         qg(5)
         tpe(6, 0)
         tev(6, "S")
-        mx(8, 0, 6)
+        mx(8, 0, 3)
         eo(8, 0, "V")
-        mx(8, 1, 7)
+        mx(8, 1, 4)
         eo(8, 1, "S")
-        mx(9, 0, 4)
+        mx(9, 0, 2)
         eo(9, 0, "V")
-        mx(9, 1, 5)
+        mx(9, 1, 1)
         eo(9, 1, "S")
         store(8, 2, 0, D_IN)
         qg(6)
-        tpe(7, 1)
+        tpe(7, 6)
         tev(7, "S")
-        mx(10, 0, 2)
+        mx(10, 0, 7)
         eo(10, 0, "V")
-        mx(10, 1, 3)
+        mx(10, 1, 5)
         eo(10, 1, "S")
-        mx(11, 0, 6)
+        mx(11, 0, 0)
         eo(11, 0, "V")
-        mx(11, 1, 7)
+        mx(11, 1, 3)
         eo(11, 1, "S")
         store(10, 2, 0, D_IN)
         qg(7)
-        tpe(8, 0)
+        tpe(8, 4)
         tev(8, "S")
-        mx(12, 0, 4)
+        mx(12, 0, 2)
         eo(12, 0, "V")
-        mx(12, 1, 5)
+        mx(12, 1, 1)
         eo(12, 1, "S")
-        mx(13, 0, 2)
+        mx(13, 0, 6)
         eo(13, 0, "V")
-        mx(13, 1, 3)
+        mx(13, 1, 7)
         eo(13, 1, "S")
         store(12, 2, 0, D_IN)
         qg(8)
-        tpe(9, 1)
+        tpe(9, 5)
         tev(9, "S")
-        mx(14, 0, 6)
+        mx(14, 0, 0)
         eo(14, 0, "V")
-        mx(14, 1, 7)
+        mx(14, 1, 3)
         eo(14, 1, "S")
         mx(15, 0, 4)
         eo(15, 0, "V")
-        mx(15, 1, 5)
+        mx(15, 1, 2)
         eo(15, 1, "S")
         store(14, 2, 0, D_IN)
         qg(9)
-        tpe(10, 0)
+        tpe(10, 1)
         tev(10, "S")
-        mx(16, 0, 2)
+        mx(16, 0, 6)
         eo(16, 0, "V")
-        mx(16, 1, 3)
+        mx(16, 1, 7)
         eo(16, 1, "S")
-        mx(17, 0, 6)
+        mx(17, 0, 5)
         eo(17, 0, "V")
-        mx(17, 1, 7)
+        mx(17, 1, 0)
         eo(17, 1, "S")
         store(16, 2, 0, D_IN)
         qg(10)
-        tpe(11, 1)
+        tpe(11, 3)
         tev(11, "S")
         mx(18, 0, 4)
         eo(18, 0, "V")
-        mx(18, 1, 5)
+        mx(18, 1, 2)
         eo(18, 1, "S")
-        mx(19, 0, 2)
+        mx(19, 0, 1)
         eo(19, 0, "V")
-        mx(19, 1, 3)
+        mx(19, 1, 6)
         eo(19, 1, "S")
         store(18, 2, 0, D_IN)
         qg(11)
-        tpe(12, 0)
+        tpe(12, 7)
         tev(12, "S")
-        mx(20, 0, 6)
+        mx(20, 0, 5)
         eo(20, 0, "V")
-        mx(20, 1, 7)
+        mx(20, 1, 0)
         eo(20, 1, "S")
-        mx(21, 0, 4)
+        mx(21, 0, 3)
         eo(21, 0, "V")
-        mx(21, 1, 5)
+        mx(21, 1, 4)
         eo(21, 1, "S")
         store(20, 2, 0, D_IN)
         qg(12)
-        tpe(13, 1)
+        tpe(13, 2)
         tev(13, "S")
-        mx(22, 0, 2)
+        mx(22, 0, 1)
         eo(22, 0, "V")
-        mx(22, 1, 3)
+        mx(22, 1, 6)
         eo(22, 1, "S")
-        mx(23, 0, 6)
+        mx(23, 0, 7)
         eo(23, 0, "V")
-        mx(23, 1, 7)
+        mx(23, 1, 5)
         eo(23, 1, "S")
         store(22, 2, 0, D_IN)
         qg(13)
         tpe(14, 0)
         tev(14, "S")
-        mx(24, 0, 4)
+        mx(24, 0, 3)
         eo(24, 0, "V")
-        mx(24, 1, 5)
+        mx(24, 1, 4)
         eo(24, 1, "S")
         mx(25, 0, 2)
         eo(25, 0, "V")
-        mx(25, 1, 3)
+        mx(25, 1, 1)
         eo(25, 1, "S")
         store(24, 2, 0, D_IN)
         qg(14)
-        tpe(15, 1)
+        tpe(15, 6)
         tev(15, "S")
-        mx(26, 0, 6)
+        mx(26, 0, 7)
         eo(26, 0, "V")
-        mx(26, 1, 7)
+        mx(26, 1, 5)
         eo(26, 1, "S")
-        mx(27, 0, 4)
+        mx(27, 0, 0)
         eo(27, 0, "V")
-        mx(27, 1, 5)
+        mx(27, 1, 3)
         eo(27, 1, "S")
         store(26, 2, 0, D_IN)
         qg(15)
-        mx(28, 0, 2)
+        mx(28, 0, 4)
         eo(28, 0, "V")
-        mx(28, 1, 3)
+        mx(28, 1, 2)
         eo(28, 1, "S")
-        mx(29, 0, 6)
+        mx(29, 0, 1)
         eo(29, 0, "V")
-        mx(29, 1, 7)
+        mx(29, 1, 6)
         eo(29, 1, "S")
         store(28, 2, 0, D_IN)
-        mx(30, 0, 4)
+        mx(30, 0, 7)
         eo(30, 0, "V")
         mx(30, 1, 5)
         eo(30, 1, "S")
-        mx(31, 0, 2)
+        mx(31, 0, 0)
         eo(31, 0, "V")
         mx(31, 1, 3)
         eo(31, 1, "S")

@@ -70,10 +70,13 @@ def tile_bitlinear_t_kernel(tc, x, weight, bias, grad_out, out):
         load_g(6, 0, 2048)
         load_g(7, 0, 2048)
 
-        ident_b = keep.tile([P, P], BF16, name="ident_b")
-        make_identity(nc, ident_b[:])
         ident_f = keep.tile([P, P], F32, name="ident_f")
         make_identity(nc, ident_f[:])
+        ident_b = keep.tile([P, P], BF16, name="ident_b")
+        make_identity(nc, ident_b[:])
+        warm = bank(7, [P, P])
+        for i in range(4):
+            nc.tensor.matmul(out=warm[:], lhsT=ident_f[:], rhs=ident_f[:], start=True, stop=True)
         two_b = keep.tile([P, P], BF16, name="two_b")
         nc.vector.tensor_scalar_mul(out=two_b[:], in0=ident_b[:], scalar1=2.0)
         neg_b = keep.tile([P, P], BF16, name="neg_b")

@@ -39,7 +39,7 @@ def tile_bitlinear_t_kernel(tc, x, weight, bias, grad_out, out):
         ctx.enter_context(tc.manual_schedule())
         keep = ctx.enter_context(tc.tile_pool(name="keep", bufs=1))
         ggp = ctx.enter_context(tc.tile_pool(name="ggp", bufs=4))
-        osp = ctx.enter_context(tc.tile_pool(name="osp", bufs=8))
+        osp = ctx.enter_context(tc.tile_pool(name="osp", bufs=5))
         psum = ctx.enter_context(tc.psum_pool(name="psum", bufs=1))
 
         def bank(b, shape):
@@ -70,13 +70,10 @@ def tile_bitlinear_t_kernel(tc, x, weight, bias, grad_out, out):
         load_g(6, 0, 2048)
         load_g(7, 0, 2048)
 
-        ident_f = keep.tile([P, P], F32, name="ident_f")
-        make_identity(nc, ident_f[:])
         ident_b = keep.tile([P, P], BF16, name="ident_b")
         make_identity(nc, ident_b[:])
-        warm = bank(7, [P, P])
-        for i in range(4):
-            nc.tensor.matmul(out=warm[:], lhsT=ident_f[:], rhs=ident_f[:], start=True, stop=True)
+        ident_f = keep.tile([P, P], F32, name="ident_f")
+        make_identity(nc, ident_f[:])
         two_b = keep.tile([P, P], BF16, name="two_b")
         nc.vector.tensor_scalar_mul(out=two_b[:], in0=ident_b[:], scalar1=2.0)
         neg_b = keep.tile([P, P], BF16, name="neg_b")
@@ -225,16 +222,16 @@ def tile_bitlinear_t_kernel(tc, x, weight, bias, grad_out, out):
             )
 
         def eo(t, h, eng):
-            grp = t // 2
+            grp = t // 4
             if grp not in ost_tiles:
-                ost_tiles[grp] = osp.tile([P, 2, D_IN], F32, name="ost")
-            copy_on(eng, ost_tiles[grp][:, t % 2, h * HALF : (h + 1) * HALF], banks["O%d_%d" % (t, h)][:])
+                ost_tiles[grp] = osp.tile([P, 4, D_IN], F32, name="ost")
+            copy_on(eng, ost_tiles[grp][:, t % 4, h * HALF : (h + 1) * HALF], banks["O%d_%d" % (t, h)][:])
 
         def store(t0, n, c0, c1):
-            grp = t0 // 2
+            grp = t0 // 4
             nc.sync.dma_start(
                 out=ov[t0 // I_SG][:, t0 % I_SG : t0 % I_SG + n, c0:c1],
-                in_=ost_tiles[grp][:, t0 % 2 : t0 % 2 + n, c0:c1],
+                in_=ost_tiles[grp][:, t0 % 4 : t0 % 4 + n, c0:c1],
             )
 
         absv(0, 0)
@@ -271,200 +268,197 @@ def tile_bitlinear_t_kernel(tc, x, weight, bias, grad_out, out):
         joinev(5, "S")
         masks(7)
         joinpe(7, 3)
-        joinev(7, "S")
         qwq(0)
-        tpe(1, 4)
-        tev(1, "S")
-        tpe(2, 5)
-        qg(0)
+        joinev(6, "S")
         qwq(1)
-        mx(0, 0, 1)
-        joinev(6, "V")
+        joinev(7, "S")
+        qg(0)
         qwq(2)
-        qwq(3)
-        mx(0, 1, 6)
-        mx(1, 0, 7)
+        tpe(1, 4)
+        tev(1, "V")
+        mx(0, 0, 5)
         eo(0, 0, "S")
+        store(0, 1, 0, 512)
+        tpe(2, 1)
+        qwq(3)
+        mx(1, 0, 6)
         qg(1)
-        eo(0, 1, "V")
-        mx(1, 1, 0)
         eo(1, 0, "S")
-        store(0, 1, 0, D_IN)
-        mx(2, 0, 3)
+        store(1, 1, 0, 512)
+        mx(0, 1, 7)
         tev(2, "V")
-        mx(2, 1, 4)
+        mx(1, 1, 0)
+        eo(0, 1, "V")
+        store(0, 1, 512, 1024)
         eo(1, 1, "S")
-        store(1, 1, 0, D_IN)
-        mx(3, 0, 2)
+        store(1, 1, 512, 1024)
+        mx(2, 0, 2)
+        mx(2, 1, 3)
+        mx(3, 0, 4)
+        mx(3, 1, 5)
+        tpe(3, 6)
         eo(2, 0, "V")
-        qg(2)
-        mx(3, 1, 1)
         eo(2, 1, "S")
+        qg(2)
         eo(3, 0, "V")
         eo(3, 1, "S")
         store(2, 2, 0, D_IN)
-        tpe(3, 6)
         tev(3, "V")
         qg(3)
-        tpe(4, 7)
+        tpe(4, 1)
         tev(4, "S")
-        mx(4, 0, 5)
+        mx(4, 0, 7)
         eo(4, 0, "V")
         mx(4, 1, 0)
         eo(4, 1, "S")
-        mx(5, 0, 3)
+        mx(5, 0, 2)
         eo(5, 0, "V")
-        mx(5, 1, 4)
+        mx(5, 1, 3)
         eo(5, 1, "S")
         store(4, 2, 0, D_IN)
         qg(4)
-        tpe(5, 2)
+        tpe(5, 4)
         tev(5, "S")
-        mx(6, 0, 1)
+        mx(6, 0, 5)
         eo(6, 0, "V")
         mx(6, 1, 6)
         eo(6, 1, "S")
-        mx(7, 0, 7)
+        mx(7, 0, 1)
         eo(7, 0, "V")
-        mx(7, 1, 5)
+        mx(7, 1, 7)
         eo(7, 1, "S")
         store(6, 2, 0, D_IN)
         qg(5)
         tpe(6, 0)
         tev(6, "S")
-        mx(8, 0, 3)
+        mx(8, 0, 2)
         eo(8, 0, "V")
-        mx(8, 1, 4)
+        mx(8, 1, 3)
         eo(8, 1, "S")
-        mx(9, 0, 2)
+        mx(9, 0, 4)
         eo(9, 0, "V")
-        mx(9, 1, 1)
+        mx(9, 1, 5)
         eo(9, 1, "S")
         store(8, 2, 0, D_IN)
         qg(6)
         tpe(7, 6)
         tev(7, "S")
-        mx(10, 0, 7)
+        mx(10, 0, 1)
         eo(10, 0, "V")
-        mx(10, 1, 5)
+        mx(10, 1, 7)
         eo(10, 1, "S")
         mx(11, 0, 0)
         eo(11, 0, "V")
-        mx(11, 1, 3)
+        mx(11, 1, 2)
         eo(11, 1, "S")
         store(10, 2, 0, D_IN)
         qg(7)
-        tpe(8, 4)
+        tpe(8, 3)
         tev(8, "S")
-        mx(12, 0, 2)
+        mx(12, 0, 4)
         eo(12, 0, "V")
-        mx(12, 1, 1)
+        mx(12, 1, 5)
         eo(12, 1, "S")
         mx(13, 0, 6)
         eo(13, 0, "V")
-        mx(13, 1, 7)
+        mx(13, 1, 1)
         eo(13, 1, "S")
-        store(12, 2, 0, D_IN)
         qg(8)
-        tpe(9, 5)
+        tpe(9, 7)
         tev(9, "S")
         mx(14, 0, 0)
         eo(14, 0, "V")
-        mx(14, 1, 3)
+        mx(14, 1, 2)
         eo(14, 1, "S")
-        mx(15, 0, 4)
+        mx(15, 0, 3)
         eo(15, 0, "V")
-        mx(15, 1, 2)
+        mx(15, 1, 4)
         eo(15, 1, "S")
-        store(14, 2, 0, D_IN)
+        store(12, 4, 0, D_IN)
         qg(9)
-        tpe(10, 1)
+        tpe(10, 5)
         tev(10, "S")
         mx(16, 0, 6)
         eo(16, 0, "V")
-        mx(16, 1, 7)
+        mx(16, 1, 1)
         eo(16, 1, "S")
-        mx(17, 0, 5)
+        mx(17, 0, 7)
         eo(17, 0, "V")
         mx(17, 1, 0)
         eo(17, 1, "S")
-        store(16, 2, 0, D_IN)
         qg(10)
-        tpe(11, 3)
+        tpe(11, 2)
         tev(11, "S")
-        mx(18, 0, 4)
+        mx(18, 0, 3)
         eo(18, 0, "V")
-        mx(18, 1, 2)
+        mx(18, 1, 4)
         eo(18, 1, "S")
-        mx(19, 0, 1)
+        mx(19, 0, 5)
         eo(19, 0, "V")
         mx(19, 1, 6)
         eo(19, 1, "S")
-        store(18, 2, 0, D_IN)
+        store(16, 4, 0, D_IN)
         qg(11)
-        tpe(12, 7)
+        tpe(12, 1)
         tev(12, "S")
-        mx(20, 0, 5)
+        mx(20, 0, 7)
         eo(20, 0, "V")
         mx(20, 1, 0)
         eo(20, 1, "S")
-        mx(21, 0, 3)
+        mx(21, 0, 2)
         eo(21, 0, "V")
-        mx(21, 1, 4)
+        mx(21, 1, 3)
         eo(21, 1, "S")
-        store(20, 2, 0, D_IN)
         qg(12)
-        tpe(13, 2)
+        tpe(13, 4)
         tev(13, "S")
-        mx(22, 0, 1)
+        mx(22, 0, 5)
         eo(22, 0, "V")
         mx(22, 1, 6)
         eo(22, 1, "S")
-        mx(23, 0, 7)
+        mx(23, 0, 1)
         eo(23, 0, "V")
-        mx(23, 1, 5)
+        mx(23, 1, 7)
         eo(23, 1, "S")
-        store(22, 2, 0, D_IN)
+        store(20, 4, 0, D_IN)
         qg(13)
         tpe(14, 0)
         tev(14, "S")
-        mx(24, 0, 3)
+        mx(24, 0, 2)
         eo(24, 0, "V")
-        mx(24, 1, 4)
+        mx(24, 1, 3)
         eo(24, 1, "S")
-        mx(25, 0, 2)
+        mx(25, 0, 4)
         eo(25, 0, "V")
-        mx(25, 1, 1)
+        mx(25, 1, 5)
         eo(25, 1, "S")
-        store(24, 2, 0, D_IN)
         qg(14)
         tpe(15, 6)
         tev(15, "S")
-        mx(26, 0, 7)
+        mx(26, 0, 1)
         eo(26, 0, "V")
-        mx(26, 1, 5)
+        mx(26, 1, 7)
         eo(26, 1, "S")
         mx(27, 0, 0)
         eo(27, 0, "V")
-        mx(27, 1, 3)
+        mx(27, 1, 2)
         eo(27, 1, "S")
-        store(26, 2, 0, D_IN)
+        store(24, 4, 0, D_IN)
         qg(15)
-        mx(28, 0, 4)
+        mx(28, 0, 3)
         eo(28, 0, "V")
-        mx(28, 1, 2)
+        mx(28, 1, 4)
         eo(28, 1, "S")
-        mx(29, 0, 1)
+        mx(29, 0, 5)
         eo(29, 0, "V")
         mx(29, 1, 6)
         eo(29, 1, "S")
-        store(28, 2, 0, D_IN)
-        mx(30, 0, 7)
+        mx(30, 0, 1)
         eo(30, 0, "V")
-        mx(30, 1, 5)
+        mx(30, 1, 7)
         eo(30, 1, "S")
         mx(31, 0, 0)
         eo(31, 0, "V")
-        mx(31, 1, 3)
+        mx(31, 1, 2)
         eo(31, 1, "S")
-        store(30, 2, 0, D_IN)
+        store(28, 4, 0, D_IN)

@@ -58,10 +58,9 @@ def tile_bitlinear_t_kernel(tc, x, weight, bias, grad_out, out):
 
         load_w(0, 0)
         load_w(0, 1)
+        load_g(0, 0, 2048)
         load_w(1, 0)
         load_w(1, 1)
-        load_g(0, 0, 1024)
-        load_g(0, 1024, 2048)
         load_g(1, 0, 2048)
         load_g(2, 0, 2048)
         load_g(3, 0, 2048)
@@ -126,13 +125,24 @@ def tile_bitlinear_t_kernel(tc, x, weight, bias, grad_out, out):
                     stop=(j == n_j - 1),
                 )
 
-        def thresholds(h):
+        def sum_folded(h, t0, t1):
             nc.vector.tensor_reduce(
-                out=sums[:, h, :],
-                in_=banks["F%d" % h][:].rearrange("p t g i -> p (t g) i"),
+                out=sums[:, h, 4 * t0 : 4 * t1],
+                in_=banks["F%d" % h][:, t0:t1, :, :].rearrange("p t g i -> p (t g) i"),
                 axis=AX.X,
                 op=ALU.add,
             )
+
+        def sum_direct(h, t0, t1):
+            nc.vector.tensor_reduce(
+                out=sums[:, h, 4 * t0 : 4 * t1],
+                in_=w2[h][:, 0, t0:t1, :].rearrange("p t (g c) -> p (t g) c", g=4),
+                axis=AX.X,
+                op=ALU.add,
+                apply_absolute_value=True,
+            )
+
+        def thresholds(h):
             nc.vector.tensor_scalar(
                 out=thr[:, h, :], in0=sums[:, h, :], scalar1=1.0 / 256, scalar2=EPS / 2,
                 op0=ALU.mult, op1=ALU.max,
@@ -236,86 +246,88 @@ def tile_bitlinear_t_kernel(tc, x, weight, bias, grad_out, out):
 
         absv(0, 0)
         fold(0, 0, 0)
-        absv(0, 1)
-        fold(0, 1, 0)
-        absv(1, 0)
-        fold(1, 0, 1)
-        abss(1, 1)
-        thresholds(0)
+        abss(0, 1)
+        sum_direct(0, 2, 4)
         tpe(0, 2)
+        tpe(1, 7)
+        sum_folded(0, 0, 2)
+        thresholds(0)
+        tev(0, "S")
         masks(0)
         joinpe(0, 3)
-        tev(0, "S")
         masks(1)
-        fold(1, 1, 1)
         joinpe(1, 4)
-        joinev(0, "S")
+        tev(1, "S")
         masks(2)
         joinpe(2, 5)
-        joinev(1, "S")
+        joinev(0, "S")
         masks(3)
         joinpe(3, 6)
+        absv(1, 0)
+        fold(1, 0, 1)
+        absv(1, 1)
+        fold(1, 1, 1)
+        joinev(1, "V")
         joinev(2, "S")
-        thresholds(1)
-        masks(4)
-        joinpe(4, 7)
-        joinev(3, "S")
-        masks(5)
-        joinpe(5, 0)
-        joinev(4, "S")
-        masks(6)
-        joinpe(6, 2)
-        joinev(5, "S")
-        masks(7)
-        joinpe(7, 3)
-        qwq(0)
-        joinev(6, "S")
-        qwq(1)
-        joinev(7, "S")
         qg(0)
-        qwq(2)
-        tpe(1, 4)
-        tev(1, "V")
-        mx(0, 0, 5)
-        eo(0, 0, "S")
-        store(0, 1, 0, 512)
-        tpe(2, 1)
-        qwq(3)
-        mx(1, 0, 6)
+        qwq(0)
         qg(1)
-        eo(1, 0, "S")
-        store(1, 1, 0, 512)
-        mx(0, 1, 7)
-        tev(2, "V")
-        mx(1, 1, 0)
-        eo(0, 1, "V")
-        store(0, 1, 512, 1024)
-        eo(1, 1, "S")
-        store(1, 1, 512, 1024)
-        mx(2, 0, 2)
-        mx(2, 1, 3)
+        tpe(2, 2)
+        joinev(3, "S")
+        tev(2, "S")
+        qwq(1)
+        mx(0, 0, 0)
+        mx(1, 0, 7)
+        mx(2, 0, 3)
         mx(3, 0, 4)
-        mx(3, 1, 5)
-        tpe(3, 6)
-        eo(2, 0, "V")
-        eo(2, 1, "S")
+        sum_folded(1, 0, 4)
+        thresholds(1)
+        eo(0, 0, "S")
+        masks(4)
+        joinpe(4, 5)
+        masks(5)
+        joinpe(5, 6)
+        eo(1, 0, "S")
+        store(0, 2, 0, 512)
+        masks(6)
+        joinpe(6, 1)
+        masks(7)
+        joinpe(7, 2)
+        eo(2, 0, "S")
         qg(2)
-        eo(3, 0, "V")
+        mx(4, 0, 0)
+        mx(5, 0, 7)
+        joinev(4, "V")
+        eo(3, 0, "S")
+        store(2, 2, 0, 512)
+        joinev(5, "V")
+        joinev(6, "S")
+        qwq(2)
+        joinev(7, "V")
+        eo(4, 0, "S")
+        qwq(3)
+        eo(5, 0, "S")
+        store(4, 2, 0, 512)
+        mx(0, 1, 3)
+        mx(1, 1, 4)
+        mx(2, 1, 5)
+        mx(3, 1, 6)
+        tpe(3, 1)
+        eo(0, 1, "V")
+        eo(1, 1, "S")
+        store(0, 2, 512, 1024)
+        eo(2, 1, "V")
         eo(3, 1, "S")
-        store(2, 2, 0, D_IN)
+        store(2, 2, 512, 1024)
         tev(3, "V")
-        qg(3)
-        tpe(4, 1)
-        tev(4, "S")
-        mx(4, 0, 7)
-        eo(4, 0, "V")
         mx(4, 1, 0)
+        mx(5, 1, 2)
+        tpe(4, 3)
         eo(4, 1, "S")
-        mx(5, 0, 2)
-        eo(5, 0, "V")
-        mx(5, 1, 3)
-        eo(5, 1, "S")
-        store(4, 2, 0, D_IN)
+        qg(3)
+        eo(5, 1, "V")
+        store(4, 2, 512, 1024)
+        tev(4, "S")
         qg(4)
         tpe(5, 4)
         tev(5, "S")

@@ -20,8 +20,9 @@ D_OUT = 512
 D_IN = 1024
 GROUP = 128
 EPS = 1e-8
-I_SG = 4
-N_SG = TOK // (P * I_SG)
+SG = (4, 4, 8, 16)
+T0 = tuple(sum(SG[:s]) for s in range(len(SG)))
+SG_OF = tuple(s for s, n in enumerate(SG) for i in range(n))
 HALF = 512
 SL = 16
 
@@ -31,8 +32,14 @@ BYTES = 2 * D_OUT * D_IN + 2 * TOK * D_OUT + 4 * TOK * D_IN
 
 def tile_bitlinear_t_kernel(tc, x, weight, bias, grad_out, out):
     nc = tc.nc
-    gv = grad_out.flatten_outer_dims().rearrange("(s p i) k -> s p (i k)", p=P, i=I_SG)
-    ov = out.flatten_outer_dims().rearrange("(s p i) c -> s p i c", p=P, i=I_SG)
+    gf = grad_out.flatten_outer_dims()
+    of = out.flatten_outer_dims()
+    gv = []
+    ov = []
+    for s, n in enumerate(SG):
+        rows = slice(T0[s] * P, (T0[s] + n) * P)
+        gv.append(gf[rows, :].rearrange("(p i) k -> p (i k)", i=n))
+        ov.append(of[rows, :].rearrange("(p i) c -> p i c", i=n))
     wv = weight.rearrange("(u q e) c -> u q e c", u=2, e=2)
 
     with ExitStack() as ctx:
@@ -46,28 +53,24 @@ def tile_bitlinear_t_kernel(tc, x, weight, bias, grad_out, out):
             return psum.tile(shape, F32, name="pb%d" % b, tag="b%d" % b)
 
         w2 = [keep.tile([P, 2, 4, HALF], BF16, name="w2_%d" % h) for h in range(2)]
-        g_sb = [keep.tile([P, I_SG * D_OUT], BF16, name="g%d" % s) for s in range(N_SG)]
+        g_sb = [keep.tile([P, n * D_OUT], BF16, name="g%d" % s) for s, n in enumerate(SG)]
 
         def load_w(h, u):
             nc.sync.dma_start(
                 out=w2[h][:, 0, 2 * u : 2 * u + 2, :], in_=wv[u][:, :, h * HALF : (h + 1) * HALF]
             )
 
-        def load_g(s, c0, c1):
-            nc.sync.dma_start(out=g_sb[s][:, c0:c1], in_=gv[s][:, c0:c1])
+        def load_g(s):
+            nc.sync.dma_start(out=g_sb[s][:], in_=gv[s])
 
         load_w(0, 0)
         load_w(0, 1)
-        load_g(0, 0, 2048)
+        load_g(0)
         load_w(1, 0)
         load_w(1, 1)
-        load_g(1, 0, 2048)
-        load_g(2, 0, 2048)
-        load_g(3, 0, 2048)
-        load_g(4, 0, 2048)
-        load_g(5, 0, 2048)
-        load_g(6, 0, 2048)
-        load_g(7, 0, 2048)
+        load_g(1)
+        load_g(2)
+        load_g(3)
 
         ident_b = keep.tile([P, P], BF16, name="ident_b")
         make_identity(nc, ident_b[:])
@@ -193,12 +196,13 @@ def tile_bitlinear_t_kernel(tc, x, weight, bias, grad_out, out):
             )
 
         def tpe(k, b):
-            g_words = g_sb[k // 2][:].bitcast(F32)
+            s = SG_OF[2 * k]
+            g_words = g_sb[s][:].bitcast(F32)
             gt = bank(b, [P, 2, 2, P])
             banks["T%d" % k] = gt
             for j in range(2):
                 for u in range(2):
-                    c0 = ((k % 2) * 2 + j) * 256 + u * P
+                    c0 = (2 * k - T0[s] + j) * 256 + u * P
                     nc.tensor.transpose(gt[:, j, u, :], g_words[:, c0 : c0 + P], ident_f[:])
 
         def tev(k, eng):
@@ -239,8 +243,9 @@ def tile_bitlinear_t_kernel(tc, x, weight, bias, grad_out, out):
 
         def store(t0, n, c0, c1):
             grp = t0 // 4
+            s = SG_OF[t0]
             nc.sync.dma_start(
-                out=ov[t0 // I_SG][:, t0 % I_SG : t0 % I_SG + n, c0:c1],
+                out=ov[s][:, t0 - T0[s] : t0 - T0[s] + n, c0:c1],
                 in_=ost_tiles[grp][:, t0 % 4 : t0 % 4 + n, c0:c1],
             )
 
@@ -351,7 +356,6 @@ def tile_bitlinear_t_kernel(tc, x, weight, bias, grad_out, out):
         eo(9, 0, "V")
         mx(9, 1, 5)
         eo(9, 1, "S")
-        store(8, 2, 0, D_IN)
         qg(6)
         tpe(7, 6)
         tev(7, "S")
@@ -363,7 +367,7 @@ def tile_bitlinear_t_kernel(tc, x, weight, bias, grad_out, out):
         eo(11, 0, "V")
         mx(11, 1, 2)
         eo(11, 1, "S")
-        store(10, 2, 0, D_IN)
+        store(8, 4, 0, D_IN)
         qg(7)
         tpe(8, 3)
         tev(8, "S")

@@ -179,6 +179,16 @@ def tile_bitlinear_t_kernel(tc, x, weight, bias, grad_out, out):
                 banks["W%d" % g][:].rearrange("p t c -> p c t"),
             )
 
+        def joinv(g):
+            nc.vector.scalar_tensor_tensor(
+                out=wg[:, g * 512 : (g + 1) * 512].rearrange("p (c t) -> p c t", t=4),
+                in0=ab[:, g, 0, :, :].rearrange("p t c -> p c t"),
+                scalar=2.0,
+                in1=ab[:, g, 1, :, :].rearrange("p t c -> p c t"),
+                op0=ALU.mult,
+                op1=ALU.subtract,
+            )
+
         def qw(h):
             cols = slice(h * HALF, (h + 1) * HALF)
             nc.vector.quantize_mx(
@@ -267,20 +277,19 @@ def tile_bitlinear_t_kernel(tc, x, weight, bias, grad_out, out):
         joinpe(2, 5)
         joinev(0, "S")
         masks(3)
-        joinpe(3, 6)
         absv(1, 0)
         fold(1, 0, 1)
+        joinv(3)
         absv(1, 1)
         fold(1, 1, 1)
-        joinev(1, "V")
+        joinev(1, "S")
         joinev(2, "S")
         qg(0)
         qwq(0)
-        qg(1)
         tpe(2, 2)
-        joinev(3, "S")
-        tev(2, "S")
+        qg(1)
         qwq(1)
+        tev(2, "S")
         mx(0, 0, 0)
         mx(1, 0, 7)
         mx(2, 0, 3)
@@ -297,7 +306,6 @@ def tile_bitlinear_t_kernel(tc, x, weight, bias, grad_out, out):
         masks(6)
         joinpe(6, 1)
         masks(7)
-        joinpe(7, 2)
         eo(2, 0, "S")
         qg(2)
         mx(4, 0, 0)
@@ -305,10 +313,10 @@ def tile_bitlinear_t_kernel(tc, x, weight, bias, grad_out, out):
         joinev(4, "V")
         eo(3, 0, "S")
         store(2, 2, 0, 512)
-        joinev(5, "V")
-        joinev(6, "S")
+        joinv(7)
+        joinev(5, "S")
+        joinev(6, "V")
         qwq(2)
-        joinev(7, "V")
         eo(4, 0, "S")
         qwq(3)
         eo(5, 0, "S")
@@ -356,6 +364,7 @@ def tile_bitlinear_t_kernel(tc, x, weight, bias, grad_out, out):
         eo(9, 0, "V")
         mx(9, 1, 5)
         eo(9, 1, "S")
+        store(8, 2, 0, D_IN)
         qg(6)
         tpe(7, 6)
         tev(7, "S")
@@ -367,7 +376,7 @@ def tile_bitlinear_t_kernel(tc, x, weight, bias, grad_out, out):
         eo(11, 0, "V")
         mx(11, 1, 2)
         eo(11, 1, "S")
-        store(8, 4, 0, D_IN)
+        store(10, 2, 0, D_IN)
         qg(7)
         tpe(8, 3)
         tev(8, "S")

@@ -72,6 +72,9 @@ def tile_bitlinear_t_kernel(tc, x, weight, bias, grad_out, out):
         load_g(2)
         load_g(3)
 
+        zero_b = keep.tile([P, HALF], BF16, name="zero_b")
+        nc.vector.memset(zero_b[:], 0.0)
+        warm_bank = psum.tile([P, HALF], F32, name="pbw", tag="b6")
         ident_b = keep.tile([P, P], BF16, name="ident_b")
         make_identity(nc, ident_b[:])
         ident_f = keep.tile([P, P], F32, name="ident_f")
@@ -81,9 +84,9 @@ def tile_bitlinear_t_kernel(tc, x, weight, bias, grad_out, out):
         neg_b = keep.tile([P, P], BF16, name="neg_b")
         nc.vector.tensor_scalar_mul(out=neg_b[:], in0=ident_b[:], scalar1=-1.0)
 
-        sums = keep.tile([P, 2, 16], F32, name="sums")
-        scale = keep.tile([P, 2, 16], F32, name="scale")
-        thr = keep.tile([P, 2, 16], F32, name="thr")
+        sums = keep.tile([P, 2, 4, 4], F32, name="sums")
+        scale = keep.tile([P, 2, 4, 4], F32, name="scale")
+        thr = keep.tile([P, 2, 4, 4], F32, name="thr")
         ab = keep.tile([P, 8, 2, 4, GROUP], BF16, name="ab")
         wg = keep.tile([P, 4 * D_IN], BF16, name="wg", align_bytes=64)
         w_codes = keep.tile([P, D_IN], U32, name="w_codes", align_bytes=64)
@@ -91,6 +94,9 @@ def tile_bitlinear_t_kernel(tc, x, weight, bias, grad_out, out):
         g_codes = keep.tile([P, TOK], U32, name="g_codes", align_bytes=64)
         g_scales = keep.tile([P, TOK], U8, name="g_scales", align_bytes=64)
 
+        outer = slice(0, 4, 3)
+        inner = slice(1, 3)
+        every = slice(0, 4)
         banks = {}
         gg_tiles = {}
         ost_tiles = {}
@@ -101,83 +107,94 @@ def tile_bitlinear_t_kernel(tc, x, weight, bias, grad_out, out):
             else:
                 nc.scalar.copy(out=dst, in_=src)
 
-        def absv(h, u):
+        def warm(src, n):
+            for j in range(n):
+                nc.tensor.matmul(out=warm_bank[:], lhsT=zero_b[:, 0:P], rhs=src, start=True, stop=True)
+
+        def absv(h, t0, t1):
             nc.vector.tensor_single_scalar(
-                out=w2[h][:].bitcast(I32)[:, 1, 2 * u : 2 * u + 2, :],
-                in_=w2[h][:].bitcast(I32)[:, 0, 2 * u : 2 * u + 2, :],
+                out=w2[h][:].bitcast(I32)[:, 1, t0:t1, :],
+                in_=w2[h][:].bitcast(I32)[:, 0, t0:t1, :],
                 scalar=0x7FFF7FFF,
                 op=ALU.bitwise_and,
             )
 
-        def abss(h, u):
-            nc.scalar.activation(
-                out=w2[h][:, 1, 2 * u : 2 * u + 2, :], in_=w2[h][:, 0, 2 * u : 2 * u + 2, :], func=ACT.Abs
-            )
+        def abss(h, t0, t1):
+            nc.scalar.activation(out=w2[h][:, 1, t0:t1, :], in_=w2[h][:, 0, t0:t1, :], func=ACT.Abs)
 
-        def fold(h, u, b):
-            if u == 0:
+        def abssum(h, t):
+            for k in range(4):
+                gs = slice(k * GROUP, (k + 1) * GROUP)
+                nc.scalar.activation(
+                    out=w2[h][:, 1, t, gs], in_=w2[h][:, 0, t, gs], func=ACT.Abs, accum_out=sums[:, h, t, k : k + 1]
+                )
+
+        def fold(h, t0, t1, b):
+            if "F%d" % h not in banks:
                 banks["F%d" % h] = bank(b, [P, 4, 4, SL])
-            src = w2[h][:, 1, 2 * u : 2 * u + 2, :].rearrange("p t (g j i) -> p t g j i", g=4, i=SL)
+            src = w2[h][:, 1, t0:t1, :].rearrange("p t (g j i) -> p t g j i", g=4, i=SL)
             n_j = GROUP // SL
             for j in range(n_j):
                 nc.tensor.matmul(
-                    out=banks["F%d" % h][:, 2 * u : 2 * u + 2, :, :],
+                    out=banks["F%d" % h][:, t0:t1, :, :],
                     lhsT=ident_b[:],
                     rhs=src[:, :, :, j, :],
                     start=(j == 0),
                     stop=(j == n_j - 1),
                 )
 
-        def sum_folded(h, t0, t1):
+        def sum_folded(h, ts):
             nc.vector.tensor_reduce(
-                out=sums[:, h, 4 * t0 : 4 * t1],
-                in_=banks["F%d" % h][:, t0:t1, :, :].rearrange("p t g i -> p (t g) i"),
+                out=sums[:, h, ts, :],
+                in_=banks["F%d" % h][:, ts, :, :],
                 axis=AX.X,
                 op=ALU.add,
             )
 
-        def sum_direct(h, t0, t1):
+        def sum_direct(h, t):
             nc.vector.tensor_reduce(
-                out=sums[:, h, 4 * t0 : 4 * t1],
-                in_=w2[h][:, 0, t0:t1, :].rearrange("p t (g c) -> p (t g) c", g=4),
+                out=sums[:, h, t, :],
+                in_=w2[h][:, 0, t, :].rearrange("p (g c) -> p g c", g=4),
                 axis=AX.X,
                 op=ALU.add,
                 apply_absolute_value=True,
             )
 
-        def thresholds(h):
+        def thresholds(h, ts):
             nc.vector.tensor_scalar(
-                out=thr[:, h, :], in0=sums[:, h, :], scalar1=1.0 / 256, scalar2=EPS / 2,
+                out=thr[:, h, ts, :], in0=sums[:, h, ts, :], scalar1=1.0 / 256, scalar2=EPS / 2,
                 op0=ALU.mult, op1=ALU.max,
             )
             nc.vector.tensor_scalar(
-                out=scale[:, h, :], in0=sums[:, h, :], scalar1=1.0 / 128, scalar2=EPS,
+                out=scale[:, h, ts, :], in0=sums[:, h, ts, :], scalar1=1.0 / 128, scalar2=EPS,
                 op0=ALU.mult, op1=ALU.max,
             )
 
-        def masks(g):
+        def masks(g, ts):
             h = g // 4
-            gs = slice((g % 4) * GROUP, (g % 4 + 1) * GROUP)
-            for t in range(4):
-                c = t * 4 + g % 4
+            k = g % 4
+            gs = slice(k * GROUP, (k + 1) * GROUP)
+            for t in ts:
                 nc.vector.tensor_scalar(
                     out=ab[:, g, :, t, :], in0=w2[h][:, :, t, gs],
-                    scalar1=thr[:, h, c : c + 1], scalar2=scale[:, h, c : c + 1],
+                    scalar1=thr[:, h, t, k : k + 1], scalar2=scale[:, h, t, k : k + 1],
                     op0=ALU.is_gt, op1=ALU.mult,
                 )
 
         def joinpe(g, b):
-            wp = bank(b, [P, 4, GROUP])
+            wp = psum.tile([P, 4 * GROUP], BF16, name="pw%d" % b, tag="b%d" % b)
             banks["W%d" % g] = wp
-            nc.tensor.matmul(out=wp[:], lhsT=two_b[:], rhs=ab[:, g, 0, :, :], start=True, stop=False)
-            nc.tensor.matmul(out=wp[:], lhsT=neg_b[:], rhs=ab[:, g, 1, :, :], start=False, stop=True)
+            for m, (coef, start) in enumerate(((two_b, True), (neg_b, False))):
+                nc.tensor.matmul(
+                    out=wp[:].rearrange("p (c t) -> p c t", t=4),
+                    lhsT=coef[:],
+                    rhs=ab[:, g, m, :, :].rearrange("p t c -> p c t"),
+                    start=start,
+                    stop=not start,
+                )
 
         def joinev(g, eng):
-            copy_on(
-                eng,
-                wg[:, g * 512 : (g + 1) * 512].rearrange("p (c t) -> p c t", t=4),
-                banks["W%d" % g][:].rearrange("p t c -> p c t"),
-            )
+            copy_on(eng, wg[:, g * 512 : (g + 1) * 512], banks["W%d" % g][:])
 
         def joinv(g):
             nc.vector.scalar_tensor_tensor(
@@ -259,231 +276,113 @@ def tile_bitlinear_t_kernel(tc, x, weight, bias, grad_out, out):
                 in_=ost_tiles[grp][:, t0 % 4 : t0 % 4 + n, c0:c1],
             )
 
-        absv(0, 0)
-        fold(0, 0, 0)
-        abss(0, 1)
-        sum_direct(0, 2, 4)
+        warm(zero_b[:], 6)
+        warm(w2[0][:, 0, 0, :], 3)
+        sum_direct(0, 0)
+        abssum(0, 1)
+        abssum(0, 2)
+        absv(0, 0, 1)
+        sum_direct(0, 3)
+        absv(0, 3, 4)
         tpe(0, 2)
         tpe(1, 7)
-        sum_folded(0, 0, 2)
-        thresholds(0)
         tev(0, "S")
-        masks(0)
+        thresholds(0, outer)
+        masks(0, (0, 3))
+        masks(1, (0, 3))
+        thresholds(0, inner)
+        masks(2, (0, 3))
+        masks(3, (0, 3))
+        masks(0, (1, 2))
         joinpe(0, 3)
-        masks(1)
+        masks(1, (1, 2))
         joinpe(1, 4)
-        tev(1, "S")
-        masks(2)
-        joinpe(2, 5)
+        masks(2, (1, 2))
+        masks(3, (1, 2))
+        abss(1, 0, 1)
+        absv(1, 1, 2)
+        fold(1, 0, 2, 0)
+        absv(1, 2, 4)
+        fold(1, 2, 4, 0)
         joinev(0, "S")
-        masks(3)
-        absv(1, 0)
-        fold(1, 0, 1)
-        joinv(3)
-        absv(1, 1)
-        fold(1, 1, 1)
+        joinv(2)
         joinev(1, "S")
-        joinev(2, "S")
-        qg(0)
-        qwq(0)
+        joinv(3)
+        tev(1, "S")
         tpe(2, 2)
-        qg(1)
+        qg(0)
         qwq(1)
+        qwq(0)
+        mx(0, 0, 1)
+        mx(1, 0, 5)
+        sum_folded(1, every)
+        qg(1)
+        thresholds(1, every)
         tev(2, "S")
-        mx(0, 0, 0)
-        mx(1, 0, 7)
+        eo(0, 0, "S")
         mx(2, 0, 3)
         mx(3, 0, 4)
-        sum_folded(1, 0, 4)
-        thresholds(1)
-        eo(0, 0, "S")
-        masks(4)
-        joinpe(4, 5)
-        masks(5)
-        joinpe(5, 6)
+        masks(4, range(4))
+        joinpe(4, 6)
         eo(1, 0, "S")
         store(0, 2, 0, 512)
-        masks(6)
-        joinpe(6, 1)
-        masks(7)
-        eo(2, 0, "S")
+        masks(5, range(4))
+        joinpe(5, 7)
         qg(2)
+        eo(2, 0, "S")
+        masks(6, range(4))
+        masks(7, range(4))
+        joinv(6)
+        joinev(4, "S")
         mx(4, 0, 0)
-        mx(5, 0, 7)
-        joinev(4, "V")
+        mx(5, 0, 2)
+        tpe(3, 6)
         eo(3, 0, "S")
         store(2, 2, 0, 512)
         joinv(7)
         joinev(5, "S")
-        joinev(6, "V")
-        qwq(2)
-        eo(4, 0, "S")
-        qwq(3)
+        tpe(4, 7)
+        eo(4, 0, "V")
         eo(5, 0, "S")
         store(4, 2, 0, 512)
-        mx(0, 1, 3)
-        mx(1, 1, 4)
-        mx(2, 1, 5)
-        mx(3, 1, 6)
-        tpe(3, 1)
-        eo(0, 1, "V")
+        qwq(2)
+        tev(3, "S")
+        qwq(3)
+        mx(0, 1, 1)
+        mx(1, 1, 5)
+        mx(2, 1, 3)
+        mx(3, 1, 4)
+        tev(4, "V")
         eo(1, 1, "S")
-        store(0, 2, 512, 1024)
-        eo(2, 1, "V")
-        eo(3, 1, "S")
-        store(2, 2, 512, 1024)
-        tev(3, "V")
-        mx(4, 1, 0)
-        mx(5, 1, 2)
-        tpe(4, 3)
-        eo(4, 1, "S")
         qg(3)
-        eo(5, 1, "V")
+        eo(0, 1, "V")
+        store(0, 2, 512, 1024)
+        mx(4, 1, 6)
+        mx(5, 1, 0)
+        eo(3, 1, "S")
+        eo(2, 1, "V")
+        store(2, 2, 512, 1024)
+        eo(5, 1, "S")
+        eo(4, 1, "V")
         store(4, 2, 512, 1024)
-        tev(4, "S")
-        qg(4)
-        tpe(5, 4)
-        tev(5, "S")
-        mx(6, 0, 5)
-        eo(6, 0, "V")
-        mx(6, 1, 6)
-        eo(6, 1, "S")
-        mx(7, 0, 1)
-        eo(7, 0, "V")
-        mx(7, 1, 7)
-        eo(7, 1, "S")
-        store(6, 2, 0, D_IN)
-        qg(5)
-        tpe(6, 0)
-        tev(6, "S")
-        mx(8, 0, 2)
-        eo(8, 0, "V")
-        mx(8, 1, 3)
-        eo(8, 1, "S")
-        mx(9, 0, 4)
-        eo(9, 0, "V")
-        mx(9, 1, 5)
-        eo(9, 1, "S")
-        store(8, 2, 0, D_IN)
-        qg(6)
-        tpe(7, 6)
-        tev(7, "S")
-        mx(10, 0, 1)
-        eo(10, 0, "V")
-        mx(10, 1, 7)
-        eo(10, 1, "S")
-        mx(11, 0, 0)
-        eo(11, 0, "V")
-        mx(11, 1, 2)
-        eo(11, 1, "S")
-        store(10, 2, 0, D_IN)
-        qg(7)
-        tpe(8, 3)
-        tev(8, "S")
-        mx(12, 0, 4)
-        eo(12, 0, "V")
-        mx(12, 1, 5)
-        eo(12, 1, "S")
-        mx(13, 0, 6)
-        eo(13, 0, "V")
-        mx(13, 1, 1)
-        eo(13, 1, "S")
-        qg(8)
-        tpe(9, 7)
-        tev(9, "S")
-        mx(14, 0, 0)
-        eo(14, 0, "V")
-        mx(14, 1, 2)
-        eo(14, 1, "S")
-        mx(15, 0, 3)
-        eo(15, 0, "V")
-        mx(15, 1, 4)
-        eo(15, 1, "S")
-        store(12, 4, 0, D_IN)
-        qg(9)
-        tpe(10, 5)
-        tev(10, "S")
-        mx(16, 0, 6)
-        eo(16, 0, "V")
-        mx(16, 1, 1)
-        eo(16, 1, "S")
-        mx(17, 0, 7)
-        eo(17, 0, "V")
-        mx(17, 1, 0)
-        eo(17, 1, "S")
-        qg(10)
-        tpe(11, 2)
-        tev(11, "S")
-        mx(18, 0, 3)
-        eo(18, 0, "V")
-        mx(18, 1, 4)
-        eo(18, 1, "S")
-        mx(19, 0, 5)
-        eo(19, 0, "V")
-        mx(19, 1, 6)
-        eo(19, 1, "S")
-        store(16, 4, 0, D_IN)
-        qg(11)
-        tpe(12, 1)
-        tev(12, "S")
-        mx(20, 0, 7)
-        eo(20, 0, "V")
-        mx(20, 1, 0)
-        eo(20, 1, "S")
-        mx(21, 0, 2)
-        eo(21, 0, "V")
-        mx(21, 1, 3)
-        eo(21, 1, "S")
-        qg(12)
-        tpe(13, 4)
-        tev(13, "S")
-        mx(22, 0, 5)
-        eo(22, 0, "V")
-        mx(22, 1, 6)
-        eo(22, 1, "S")
-        mx(23, 0, 1)
-        eo(23, 0, "V")
-        mx(23, 1, 7)
-        eo(23, 1, "S")
-        store(20, 4, 0, D_IN)
-        qg(13)
-        tpe(14, 0)
-        tev(14, "S")
-        mx(24, 0, 2)
-        eo(24, 0, "V")
-        mx(24, 1, 3)
-        eo(24, 1, "S")
-        mx(25, 0, 4)
-        eo(25, 0, "V")
-        mx(25, 1, 5)
-        eo(25, 1, "S")
-        qg(14)
-        tpe(15, 6)
-        tev(15, "S")
-        mx(26, 0, 1)
-        eo(26, 0, "V")
-        mx(26, 1, 7)
-        eo(26, 1, "S")
-        mx(27, 0, 0)
-        eo(27, 0, "V")
-        mx(27, 1, 2)
-        eo(27, 1, "S")
-        store(24, 4, 0, D_IN)
-        qg(15)
-        mx(28, 0, 3)
-        eo(28, 0, "V")
-        mx(28, 1, 4)
-        eo(28, 1, "S")
-        mx(29, 0, 5)
-        eo(29, 0, "V")
-        mx(29, 1, 6)
-        eo(29, 1, "S")
-        mx(30, 0, 1)
-        eo(30, 0, "V")
-        mx(30, 1, 7)
-        eo(30, 1, "S")
-        mx(31, 0, 0)
-        eo(31, 0, "V")
-        mx(31, 1, 2)
-        eo(31, 1, "S")
-        store(28, 4, 0, D_IN)
+        order = (2, 7, 1, 5, 3, 4, 6, 0)
+        used = []
+
+        def next_bank():
+            used.append(order[len(used) % 8])
+            return used[-1]
+
+        for k in range(3, 16):
+            if k < 15:
+                qg(k + 1)
+            if k < 14:
+                tpe(k + 2, next_bank())
+                tev(k + 2, "S")
+            for t in (2 * k, 2 * k + 1):
+                for h in range(2):
+                    mx(t, h, next_bank())
+                    eo(t, h, "VS"[h])
+            if k < 6:
+                store(2 * k, 2, 0, D_IN)
+            elif k % 2 == 1:
+                store(2 * k - 2, 4, 0, D_IN)

@@ -182,19 +182,17 @@ def tile_bitlinear_t_kernel(tc, x, weight, bias, grad_out, out):
                 )
 
         def joinpe(g, b):
-            wp = psum.tile([P, 4 * GROUP], BF16, name="pw%d" % b, tag="b%d" % b)
+            wp = bank(b, [P, 4, GROUP])
             banks["W%d" % g] = wp
-            for m, (coef, start) in enumerate(((two_b, True), (neg_b, False))):
-                nc.tensor.matmul(
-                    out=wp[:].rearrange("p (c t) -> p c t", t=4),
-                    lhsT=coef[:],
-                    rhs=ab[:, g, m, :, :].rearrange("p t c -> p c t"),
-                    start=start,
-                    stop=not start,
-                )
+            nc.tensor.matmul(out=wp[:], lhsT=two_b[:], rhs=ab[:, g, 0, :, :], start=True, stop=False)
+            nc.tensor.matmul(out=wp[:], lhsT=neg_b[:], rhs=ab[:, g, 1, :, :], start=False, stop=True)
 
         def joinev(g, eng):
-            copy_on(eng, wg[:, g * 512 : (g + 1) * 512], banks["W%d" % g][:])
+            copy_on(
+                eng,
+                wg[:, g * 512 : (g + 1) * 512].rearrange("p (c t) -> p c t", t=4),
+                banks["W%d" % g][:].rearrange("p t c -> p c t"),
+            )
 
         def joinv(g):
             nc.vector.scalar_tensor_tensor(

@@ -274,8 +274,8 @@ def tile_bitlinear_t_kernel(tc, x, weight, bias, grad_out, out):
                 in_=ost_tiles[grp][:, t0 % 4 : t0 % 4 + n, c0:c1],
             )
 
-        warm(zero_b[:], 6)
-        warm(w2[0][:, 0, 0, :], 3)
+        warm(zero_b[:], 5)
+        warm(w2[0][:, 0, 0, :], 2)
         sum_direct(0, 0)
         abssum(0, 1)
         abssum(0, 2)
@@ -296,21 +296,22 @@ def tile_bitlinear_t_kernel(tc, x, weight, bias, grad_out, out):
         masks(1, (1, 2))
         joinpe(1, 4)
         masks(2, (1, 2))
+        joinpe(2, 5)
         masks(3, (1, 2))
         abss(1, 0, 1)
         absv(1, 1, 2)
         fold(1, 0, 2, 0)
         absv(1, 2, 4)
         fold(1, 2, 4, 0)
-        joinev(0, "S")
-        joinv(2)
-        joinev(1, "S")
         joinv(3)
+        joinev(0, "S")
+        joinev(1, "S")
         tev(1, "S")
         tpe(2, 2)
         qg(0)
-        qwq(1)
+        joinev(2, "V")
         qwq(0)
+        qwq(1)
         mx(0, 0, 1)
         mx(1, 0, 5)
         sum_folded(1, every)
@@ -329,23 +330,25 @@ def tile_bitlinear_t_kernel(tc, x, weight, bias, grad_out, out):
         qg(2)
         eo(2, 0, "S")
         masks(6, range(4))
+        joinpe(6, 1)
         masks(7, range(4))
-        joinv(6)
-        joinev(4, "S")
-        mx(4, 0, 0)
-        mx(5, 0, 2)
-        tpe(3, 6)
+        joinpe(7, 5)
         eo(3, 0, "S")
         store(2, 2, 0, 512)
-        joinv(7)
+        mx(4, 0, 0)
+        mx(5, 0, 2)
+        joinev(4, "V")
         joinev(5, "S")
+        tpe(3, 6)
         tpe(4, 7)
+        joinev(6, "V")
+        qwq(2)
+        joinev(7, "S")
         eo(4, 0, "V")
         eo(5, 0, "S")
         store(4, 2, 0, 512)
-        qwq(2)
-        tev(3, "S")
         qwq(3)
+        tev(3, "S")
         mx(0, 1, 1)
         mx(1, 1, 5)
         mx(2, 1, 3)

@@ -275,7 +275,7 @@ def tile_bitlinear_t_kernel(tc, x, weight, bias, grad_out, out):
             )
 
         warm(zero_b[:], 5)
-        warm(w2[0][:, 0, 0, :], 2)
+        warm(w2[0][:, 0, 0, :], 3)
         sum_direct(0, 0)
         abssum(0, 1)
         abssum(0, 2)
@@ -332,39 +332,41 @@ def tile_bitlinear_t_kernel(tc, x, weight, bias, grad_out, out):
         masks(6, range(4))
         joinpe(6, 1)
         masks(7, range(4))
-        joinpe(7, 5)
-        eo(3, 0, "S")
-        store(2, 2, 0, 512)
+        store(2, 1, 0, 512)
+        joinev(4, "S")
         mx(4, 0, 0)
         mx(5, 0, 2)
-        joinev(4, "V")
+        joinv(7)
         joinev(5, "S")
         tpe(3, 6)
         tpe(4, 7)
         joinev(6, "V")
+        eo(3, 0, "S")
+        store(3, 1, 0, 512)
         qwq(2)
-        joinev(7, "S")
-        eo(4, 0, "V")
-        eo(5, 0, "S")
-        store(4, 2, 0, 512)
         qwq(3)
+        eo(4, 0, "V")
+        store(4, 1, 0, 512)
+        eo(5, 0, "S")
+        store(5, 1, 0, 512)
         tev(3, "S")
         mx(0, 1, 1)
         mx(1, 1, 5)
         mx(2, 1, 3)
         mx(3, 1, 4)
+        eo(0, 1, "S")
+        store(0, 1, 512, 1024)
         tev(4, "V")
-        eo(1, 1, "S")
         qg(3)
-        eo(0, 1, "V")
-        store(0, 2, 512, 1024)
+        eo(1, 1, "V")
+        store(1, 1, 512, 1024)
         mx(4, 1, 6)
         mx(5, 1, 0)
-        eo(3, 1, "S")
-        eo(2, 1, "V")
+        eo(2, 1, "S")
+        eo(3, 1, "V")
         store(2, 2, 512, 1024)
-        eo(5, 1, "S")
-        eo(4, 1, "V")
+        eo(4, 1, "S")
+        eo(5, 1, "V")
         store(4, 2, 512, 1024)
         order = (2, 7, 1, 5, 3, 4, 6, 0)
         used = []

@@ -20,7 +20,8 @@ D_OUT = 512
 D_IN = 1024
 GROUP = 128
 EPS = 1e-8
-SG = (4, 4, 8, 16)
+SG = (4, 4, 24)
+CHUNKS = ((0, 4), (4, 2), (6, 2), (8, 2), (10, 4), (14, 4), (18, 6), (24, 8))
 T0 = tuple(sum(SG[:s]) for s in range(len(SG)))
 SG_OF = tuple(s for s, n in enumerate(SG) for i in range(n))
 HALF = 512
@@ -46,7 +47,6 @@ def tile_bitlinear_t_kernel(tc, x, weight, bias, grad_out, out):
         ctx.enter_context(tc.manual_schedule())
         keep = ctx.enter_context(tc.tile_pool(name="keep", bufs=1))
         ggp = ctx.enter_context(tc.tile_pool(name="ggp", bufs=4))
-        osp = ctx.enter_context(tc.tile_pool(name="osp", bufs=5))
         psum = ctx.enter_context(tc.psum_pool(name="psum", bufs=1))
 
         def bank(b, shape):
@@ -70,7 +70,6 @@ def tile_bitlinear_t_kernel(tc, x, weight, bias, grad_out, out):
         load_w(1, 1)
         load_g(1)
         load_g(2)
-        load_g(3)
 
         zero_b = keep.tile([P, HALF], BF16, name="zero_b")
         nc.vector.memset(zero_b[:], 0.0)
@@ -99,7 +98,11 @@ def tile_bitlinear_t_kernel(tc, x, weight, bias, grad_out, out):
         every = slice(0, 4)
         banks = {}
         gg_tiles = {}
-        ost_tiles = {}
+        ost = {}
+        for t0, n in CHUNKS:
+            chunk = keep.tile([P, n, D_IN], F32, name="ost%d" % t0)
+            for i in range(n):
+                ost[t0 + i] = (chunk, i)
 
         def copy_on(eng, dst, src):
             if eng == "V":
@@ -261,18 +264,13 @@ def tile_bitlinear_t_kernel(tc, x, weight, bias, grad_out, out):
             )
 
         def eo(t, h, eng):
-            grp = t // 4
-            if grp not in ost_tiles:
-                ost_tiles[grp] = osp.tile([P, 4, D_IN], F32, name="ost")
-            copy_on(eng, ost_tiles[grp][:, t % 4, h * HALF : (h + 1) * HALF], banks["O%d_%d" % (t, h)][:])
+            chunk, i = ost[t]
+            copy_on(eng, chunk[:, i, h * HALF : (h + 1) * HALF], banks["O%d_%d" % (t, h)][:])
 
         def store(t0, n, c0, c1):
-            grp = t0 // 4
+            chunk, i = ost[t0]
             s = SG_OF[t0]
-            nc.sync.dma_start(
-                out=ov[s][:, t0 - T0[s] : t0 - T0[s] + n, c0:c1],
-                in_=ost_tiles[grp][:, t0 % 4 : t0 % 4 + n, c0:c1],
-            )
+            nc.sync.dma_start(out=ov[s][:, t0 - T0[s] : t0 - T0[s] + n, c0:c1], in_=chunk[:, i : i + n, c0:c1])
 
         warm(zero_b[:], 5)
         warm(w2[0][:, 0, 0, :], 3)
@@ -332,7 +330,6 @@ def tile_bitlinear_t_kernel(tc, x, weight, bias, grad_out, out):
         masks(6, range(4))
         joinpe(6, 1)
         masks(7, range(4))
-        store(2, 1, 0, 512)
         joinev(4, "S")
         mx(4, 0, 0)
         mx(5, 0, 2)
@@ -340,33 +337,31 @@ def tile_bitlinear_t_kernel(tc, x, weight, bias, grad_out, out):
         joinev(5, "S")
         tpe(3, 6)
         tpe(4, 7)
-        joinev(6, "V")
         eo(3, 0, "S")
-        store(3, 1, 0, 512)
+        store(2, 2, 0, 512)
+        joinev(6, "V")
         qwq(2)
         qwq(3)
         eo(4, 0, "V")
-        store(4, 1, 0, 512)
         eo(5, 0, "S")
-        store(5, 1, 0, 512)
+        store(4, 2, 0, 512)
         tev(3, "S")
         mx(0, 1, 1)
         mx(1, 1, 5)
         mx(2, 1, 3)
         mx(3, 1, 4)
-        eo(0, 1, "S")
-        store(0, 1, 512, 1024)
         tev(4, "V")
+        eo(1, 1, "S")
         qg(3)
-        eo(1, 1, "V")
-        store(1, 1, 512, 1024)
+        eo(0, 1, "V")
+        store(0, 2, 512, 1024)
         mx(4, 1, 6)
         mx(5, 1, 0)
-        eo(2, 1, "S")
-        eo(3, 1, "V")
+        eo(3, 1, "S")
+        eo(2, 1, "V")
         store(2, 2, 512, 1024)
-        eo(4, 1, "S")
-        eo(5, 1, "V")
+        eo(5, 1, "S")
+        eo(4, 1, "V")
         store(4, 2, 512, 1024)
         order = (2, 7, 1, 5, 3, 4, 6, 0)
         used = []
@@ -385,7 +380,6 @@ def tile_bitlinear_t_kernel(tc, x, weight, bias, grad_out, out):
                 for h in range(2):
                     mx(t, h, next_bank())
                     eo(t, h, "VS"[h])
-            if k < 6:
-                store(2 * k, 2, 0, D_IN)
-            elif k % 2 == 1:
-                store(2 * k - 2, 4, 0, D_IN)
+            for t0, n in CHUNKS:
+                if t0 + n == 2 * k + 2:
+                    store(t0, n, 0, D_IN)

@@ -20,8 +20,8 @@ D_OUT = 512
 D_IN = 1024
 GROUP = 128
 EPS = 1e-8
-SG = (4, 4, 24)
-CHUNKS = ((0, 4), (4, 2), (6, 2), (8, 2), (10, 4), (14, 4), (18, 6), (24, 8))
+SG = (4, 4, 8, 16)
+CHUNKS = ((0, 4), (4, 2), (6, 2), (8, 2), (10, 2), (12, 4), (16, 4), (20, 4), (24, 8))
 T0 = tuple(sum(SG[:s]) for s in range(len(SG)))
 SG_OF = tuple(s for s, n in enumerate(SG) for i in range(n))
 HALF = 512
@@ -70,6 +70,7 @@ def tile_bitlinear_t_kernel(tc, x, weight, bias, grad_out, out):
         load_w(1, 1)
         load_g(1)
         load_g(2)
+        load_g(3)
 
         zero_b = keep.tile([P, HALF], BF16, name="zero_b")
         nc.vector.memset(zero_b[:], 0.0)
@@ -333,35 +334,36 @@ def tile_bitlinear_t_kernel(tc, x, weight, bias, grad_out, out):
         joinev(4, "S")
         mx(4, 0, 0)
         mx(5, 0, 2)
+        eo(3, 0, "V")
+        store(2, 2, 0, 512)
         joinv(7)
         joinev(5, "S")
         tpe(3, 6)
         tpe(4, 7)
-        eo(3, 0, "S")
-        store(2, 2, 0, 512)
         joinev(6, "V")
         qwq(2)
         qwq(3)
-        eo(4, 0, "V")
+        eo(4, 0, "S")
         eo(5, 0, "S")
         store(4, 2, 0, 512)
-        tev(3, "S")
+        tev(3, "V")
         mx(0, 1, 1)
         mx(1, 1, 5)
         mx(2, 1, 3)
         mx(3, 1, 4)
+        eo(0, 1, "S")
+        store(0, 1, 512, 1024)
         tev(4, "V")
         eo(1, 1, "S")
+        store(1, 1, 512, 1024)
         qg(3)
-        eo(0, 1, "V")
-        store(0, 2, 512, 1024)
         mx(4, 1, 6)
         mx(5, 1, 0)
-        eo(3, 1, "S")
         eo(2, 1, "V")
+        eo(3, 1, "S")
         store(2, 2, 512, 1024)
-        eo(5, 1, "S")
         eo(4, 1, "V")
+        eo(5, 1, "S")
         store(4, 2, 512, 1024)
         order = (2, 7, 1, 5, 3, 4, 6, 0)
         used = []

from contextlib import ExitStack

import concourse.mybir as mybir
from concourse.masks import make_identity

F32 = mybir.dt.float32
BF16 = mybir.dt.bfloat16
I32 = mybir.dt.int32
U32 = mybir.dt.uint32
U8 = mybir.dt.uint8
E4 = mybir.dt.float8_e4m3fn_x4
E5 = mybir.dt.float8_e5m2_x4
ALU = mybir.AluOpType
ACT = mybir.ActivationFunctionType
AX = mybir.AxisListType

P = 128
TOK = 4096
D_OUT = 512
D_IN = 1024
GROUP = 128
EPS = 1e-8
SG = (4, 4, 8, 16)
CHUNKS = ((0, 4), (4, 2), (6, 2), (8, 2), (10, 2), (12, 4), (16, 4), (20, 4), (24, 8))
T0 = tuple(sum(SG[:s]) for s in range(len(SG)))
SG_OF = tuple(s for s, n in enumerate(SG) for i in range(n))
HALF = 512
SL = 16

FLOPS = 2 * TOK * D_OUT * D_IN
BYTES = 2 * D_OUT * D_IN + 2 * TOK * D_OUT + 4 * TOK * D_IN


def tile_bitlinear_t_kernel(tc, x, weight, bias, grad_out, out):
    nc = tc.nc
    gf = grad_out.flatten_outer_dims()
    of = out.flatten_outer_dims()
    gv = []
    ov = []
    for s, n in enumerate(SG):
        rows = slice(T0[s] * P, (T0[s] + n) * P)
        gv.append(gf[rows, :].rearrange("(p i) k -> p (i k)", i=n))
        ov.append(of[rows, :].rearrange("(p i) c -> p i c", i=n))
    wv = weight.rearrange("(u q e) c -> u q e c", u=2, e=2)

    with ExitStack() as ctx:
        ctx.enter_context(tc.manual_schedule())
        keep = ctx.enter_context(tc.tile_pool(name="keep", bufs=1))
        ggp = ctx.enter_context(tc.tile_pool(name="ggp", bufs=4))
        psum = ctx.enter_context(tc.psum_pool(name="psum", bufs=1))

        def bank(b, shape):
            return psum.tile(shape, F32, name="pb%d" % b, tag="b%d" % b)

        w2 = [keep.tile([P, 2, 4, HALF], BF16, name="w2_%d" % h) for h in range(2)]
        g_sb = [keep.tile([P, n * D_OUT], BF16, name="g%d" % s) for s, n in enumerate(SG)]

        def load_w(h, u):
            nc.sync.dma_start(
                out=w2[h][:, 0, 2 * u : 2 * u + 2, :], in_=wv[u][:, :, h * HALF : (h + 1) * HALF]
            )

        def load_g(s):
            nc.sync.dma_start(out=g_sb[s][:], in_=gv[s])

        load_w(0, 0)
        load_w(0, 1)
        load_g(0)
        load_w(1, 0)
        load_w(1, 1)
        load_g(1)
        load_g(2)
        load_g(3)

        zero_b = keep.tile([P, HALF], BF16, name="zero_b")
        nc.vector.memset(zero_b[:], 0.0)
        warm_bank = psum.tile([P, HALF], F32, name="pbw", tag="b6")
        ident_b = keep.tile([P, P], BF16, name="ident_b")
        make_identity(nc, ident_b[:])
        ident_f = keep.tile([P, P], F32, name="ident_f")
        make_identity(nc, ident_f[:])
        two_b = keep.tile([P, P], BF16, name="two_b")
        nc.vector.tensor_scalar_mul(out=two_b[:], in0=ident_b[:], scalar1=2.0)
        neg_b = keep.tile([P, P], BF16, name="neg_b")
        nc.vector.tensor_scalar_mul(out=neg_b[:], in0=ident_b[:], scalar1=-1.0)

        sums = keep.tile([P, 2, 4, 4], F32, name="sums")
        scale = keep.tile([P, 2, 4, 4], F32, name="scale")
        thr = keep.tile([P, 2, 4, 4], F32, name="thr")
        ab = keep.tile([P, 8, 2, 4, GROUP], BF16, name="ab")
        wg = keep.tile([P, 4 * D_IN], BF16, name="wg", align_bytes=64)
        w_codes = keep.tile([P, D_IN], U32, name="w_codes", align_bytes=64)
        w_scales = keep.tile([P, D_IN], U8, name="w_scales", align_bytes=64)
        g_codes = keep.tile([P, TOK], U32, name="g_codes", align_bytes=64)
        g_scales = keep.tile([P, TOK], U8, name="g_scales", align_bytes=64)

        outer = slice(0, 4, 3)
        inner = slice(1, 3)
        every = slice(0, 4)
        banks = {}
        gg_tiles = {}
        ost = {}
        for t0, n in CHUNKS:
            chunk = keep.tile([P, n, D_IN], F32, name="ost%d" % t0)
            for i in range(n):
                ost[t0 + i] = (chunk, i)

        def copy_on(eng, dst, src):
            if eng == "V":
                nc.vector.tensor_copy(out=dst, in_=src)
            else:
                nc.scalar.copy(out=dst, in_=src)

        def warm(src, n):
            for j in range(n):
                nc.tensor.matmul(out=warm_bank[:], lhsT=zero_b[:, 0:P], rhs=src, start=True, stop=True)

        def absv(h, t0, t1):
            nc.vector.tensor_single_scalar(
                out=w2[h][:].bitcast(I32)[:, 1, t0:t1, :],
                in_=w2[h][:].bitcast(I32)[:, 0, t0:t1, :],
                scalar=0x7FFF7FFF,
                op=ALU.bitwise_and,
            )

        def abss(h, t0, t1):
            nc.scalar.activation(out=w2[h][:, 1, t0:t1, :], in_=w2[h][:, 0, t0:t1, :], func=ACT.Abs)

        def abssum(h, t):
            for k in range(4):
                gs = slice(k * GROUP, (k + 1) * GROUP)
                nc.scalar.activation(
                    out=w2[h][:, 1, t, gs], in_=w2[h][:, 0, t, gs], func=ACT.Abs, accum_out=sums[:, h, t, k : k + 1]
                )

        def fold(h, t0, t1, b):
            if "F%d" % h not in banks:
                banks["F%d" % h] = bank(b, [P, 4, 4, SL])
            src = w2[h][:, 1, t0:t1, :].rearrange("p t (g j i) -> p t g j i", g=4, i=SL)
            n_j = GROUP // SL
            for j in range(n_j):
                nc.tensor.matmul(
                    out=banks["F%d" % h][:, t0:t1, :, :],
                    lhsT=ident_b[:],
                    rhs=src[:, :, :, j, :],
                    start=(j == 0),
                    stop=(j == n_j - 1),
                )

        def sum_folded(h, ts):
            nc.vector.tensor_reduce(
                out=sums[:, h, ts, :],
                in_=banks["F%d" % h][:, ts, :, :],
                axis=AX.X,
                op=ALU.add,
            )

        def sum_direct(h, t):
            nc.vector.tensor_reduce(
                out=sums[:, h, t, :],
                in_=w2[h][:, 0, t, :].rearrange("p (g c) -> p g c", g=4),
                axis=AX.X,
                op=ALU.add,
                apply_absolute_value=True,
            )

        def thresholds(h, ts):
            nc.vector.tensor_scalar(
                out=thr[:, h, ts, :], in0=sums[:, h, ts, :], scalar1=1.0 / 256, scalar2=EPS / 2,
                op0=ALU.mult, op1=ALU.max,
            )
            nc.vector.tensor_scalar(
                out=scale[:, h, ts, :], in0=sums[:, h, ts, :], scalar1=1.0 / 128, scalar2=EPS,
                op0=ALU.mult, op1=ALU.max,
            )

        def masks(g, ts):
            h = g // 4
            k = g % 4
            gs = slice(k * GROUP, (k + 1) * GROUP)
            for t in ts:
                nc.vector.tensor_scalar(
                    out=ab[:, g, :, t, :], in0=w2[h][:, :, t, gs],
                    scalar1=thr[:, h, t, k : k + 1], scalar2=scale[:, h, t, k : k + 1],
                    op0=ALU.is_gt, op1=ALU.mult,
                )

        def joinpe(g, b):
            wp = bank(b, [P, 4, GROUP])
            banks["W%d" % g] = wp
            nc.tensor.matmul(out=wp[:], lhsT=two_b[:], rhs=ab[:, g, 0, :, :], start=True, stop=False)
            nc.tensor.matmul(out=wp[:], lhsT=neg_b[:], rhs=ab[:, g, 1, :, :], start=False, stop=True)

        def joinev(g, eng):
            copy_on(
                eng,
                wg[:, g * 512 : (g + 1) * 512].rearrange("p (c t) -> p c t", t=4),
                banks["W%d" % g][:].rearrange("p t c -> p c t"),
            )

        def joinv(g):
            nc.vector.scalar_tensor_tensor(
                out=wg[:, g * 512 : (g + 1) * 512].rearrange("p (c t) -> p c t", t=4),
                in0=ab[:, g, 0, :, :].rearrange("p t c -> p c t"),
                scalar=2.0,
                in1=ab[:, g, 1, :, :].rearrange("p t c -> p c t"),
                op0=ALU.mult,
                op1=ALU.subtract,
            )

        def qw(h):
            cols = slice(h * HALF, (h + 1) * HALF)
            nc.vector.quantize_mx(
                out=w_codes[:, cols].bitcast(E4),
                scales=w_scales[:, cols],
                in_=wg[:, h * 2048 : (h + 1) * 2048],
            )

        def qwq(i):
            cols = slice(i * 256, (i + 1) * 256)
            nc.vector.quantize_mx(
                out=w_codes[:, cols].bitcast(E4),
                scales=w_scales[:, cols],
                in_=wg[:, i * 1024 : (i + 1) * 1024],
            )

        def tpe(k, b):
            s = SG_OF[2 * k]
            g_words = g_sb[s][:].bitcast(F32)
            gt = bank(b, [P, 2, 2, P])
            banks["T%d" % k] = gt
            for j in range(2):
                for u in range(2):
                    c0 = (2 * k - T0[s] + j) * 256 + u * P
                    nc.tensor.transpose(gt[:, j, u, :], g_words[:, c0 : c0 + P], ident_f[:])

        def tev(k, eng):
            gg = ggp.tile([P, 2 * D_OUT], BF16, name="gg", align_bytes=64)
            gg_tiles[k] = gg
            copy_on(
                eng,
                gg[:].bitcast(F32).rearrange("p (j r u) -> p j r u", j=2, u=2),
                banks["T%d" % k][:].rearrange("p j u r -> p j r u"),
            )

        def qg(k):
            cols = slice(k * 256, (k + 1) * 256)
            nc.vector.quantize_mx(
                out=g_codes[:, cols].bitcast(E5), scales=g_scales[:, cols], in_=gg_tiles[k][:]
            )

        def mx(t, h, b):
            tcols = slice(t * P, (t + 1) * P)
            hcols = slice(h * HALF, (h + 1) * HALF)
            po = bank(b, [P, HALF])
            banks["O%d_%d" % (t, h)] = po
            nc.tensor.matmul_mx(
                out=po[:],
                lhsT=g_codes[:, tcols].bitcast(E5),
                lhsT_scale=g_scales[:, tcols],
                rhs=w_codes[:, hcols].bitcast(E4),
                rhs_scale=w_scales[:, hcols],
                start=True,
                stop=True,
            )

        def eo(t, h, eng):
            chunk, i = ost[t]
            copy_on(eng, chunk[:, i, h * HALF : (h + 1) * HALF], banks["O%d_%d" % (t, h)][:])

        def store(t0, n, c0, c1):
            chunk, i = ost[t0]
            s = SG_OF[t0]
            nc.sync.dma_start(out=ov[s][:, t0 - T0[s] : t0 - T0[s] + n, c0:c1], in_=chunk[:, i : i + n, c0:c1])

        warm(zero_b[:], 5)
        warm(w2[0][:, 0, 0, :], 3)
        sum_direct(0, 0)
        abssum(0, 1)
        abssum(0, 2)
        absv(0, 0, 1)
        sum_direct(0, 3)
        absv(0, 3, 4)
        tpe(0, 2)
        tpe(1, 7)
        tev(0, "S")
        thresholds(0, outer)
        masks(0, (0, 3))
        masks(1, (0, 3))
        thresholds(0, inner)
        masks(2, (0, 3))
        masks(3, (0, 3))
        masks(0, (1, 2))
        joinpe(0, 3)
        masks(1, (1, 2))
        joinpe(1, 4)
        masks(2, (1, 2))
        joinpe(2, 5)
        masks(3, (1, 2))
        abss(1, 0, 1)
        absv(1, 1, 2)
        fold(1, 0, 2, 0)
        absv(1, 2, 4)
        fold(1, 2, 4, 0)
        joinv(3)
        joinev(0, "S")
        joinev(1, "S")
        tev(1, "S")
        tpe(2, 2)
        qg(0)
        joinev(2, "V")
        qwq(0)
        qwq(1)
        mx(0, 0, 1)
        mx(1, 0, 5)
        sum_folded(1, every)
        qg(1)
        thresholds(1, every)
        tev(2, "S")
        eo(0, 0, "S")
        mx(2, 0, 3)
        mx(3, 0, 4)
        masks(4, range(4))
        joinpe(4, 6)
        eo(1, 0, "S")
        store(0, 2, 0, 512)
        masks(5, range(4))
        joinpe(5, 7)
        qg(2)
        eo(2, 0, "S")
        masks(6, range(4))
        joinpe(6, 1)
        masks(7, range(4))
        joinev(4, "S")
        mx(4, 0, 0)
        mx(5, 0, 2)
        eo(3, 0, "V")
        store(2, 2, 0, 512)
        joinv(7)
        joinev(5, "S")
        tpe(3, 6)
        tpe(4, 7)
        joinev(6, "V")
        qwq(2)
        qwq(3)
        eo(4, 0, "S")
        eo(5, 0, "S")
        store(4, 2, 0, 512)
        tev(3, "V")
        mx(0, 1, 1)
        mx(1, 1, 5)
        mx(2, 1, 3)
        mx(3, 1, 4)
        eo(0, 1, "S")
        store(0, 1, 512, 1024)
        tev(4, "V")
        eo(1, 1, "S")
        store(1, 1, 512, 1024)
        qg(3)
        mx(4, 1, 6)
        mx(5, 1, 0)
        eo(2, 1, "V")
        eo(3, 1, "S")
        store(2, 2, 512, 1024)
        eo(4, 1, "V")
        eo(5, 1, "S")
        store(4, 2, 512, 1024)
        order = (2, 7, 1, 5, 3, 4, 6, 0)
        used = []

        def next_bank():
            used.append(order[len(used) % 8])
            return used[-1]

        for k in range(3, 16):
            if k < 15:
                qg(k + 1)
            if k < 14:
                tpe(k + 2, next_bank())
                tev(k + 2, "S")
            for t in (2 * k, 2 * k + 1):
                for h in range(2):
                    mx(t, h, next_bank())
                    eo(t, h, "VS"[h])
            for t0, n in CHUNKS:
                if t0 + n == 2 * k + 2:
                    store(t0, n, 0, D_IN)
